import numpy as np
import ml_dtypes


def mxq(x, axis, fmt="e4m3"):
    dtype, down = {"e4m3": (ml_dtypes.float8_e4m3fn, 7), "e5m2": (ml_dtypes.float8_e5m2, 14)}[fmt]
    v = np.moveaxis(np.asarray(x, np.float32).astype(ml_dtypes.bfloat16).astype(np.float64), axis, -1)
    blocks = v.reshape(v.shape[:-1] + (-1, 32))
    amax = np.abs(blocks).max(-1, keepdims=True)
    byte = np.maximum(np.where(amax > 0, np.frexp(amax)[1] - 1 + 127, 0) - down, 1)
    scale = np.exp2(byte - 127.0)
    codes = (blocks / scale).astype(np.float32).astype(dtype).astype(np.float64)
    return np.moveaxis((codes * scale).reshape(v.shape), -1, axis)


WIDE = False


def mx_kscale(k):
    if not WIDE:
        return np.ones(k)
    levels = np.array([10, -10, 5, -5, 0])
    if k % 512:
        return np.exp2(np.random.permutation(np.resize(levels, k // 32))).repeat(32)
    a = np.empty((k // 512, 16))
    for p in range(k // 512):
        a[p, :8] = np.random.permutation(np.resize(levels, 8))
        for g in range(8):
            far = levels[np.abs(levels - a[p, g]) >= 10]
            a[p, g + 8] = far[np.random.randint(len(far))]
    return np.exp2(a.ravel()).repeat(32)


BF16 = ml_dtypes.bfloat16


def bf(x):
    return np.asarray(x, np.float32).astype(BF16)


def f64(x):
    return np.asarray(x).astype(np.float64)


BS, NF, N, J, NOUT = 8, 512, 512, 3, 128
KC = J * NF
EPS = 1e-5


def setup_inputs():
    s = mx_kscale(N)
    c = mx_kscale(NF)
    t = np.tile(c, J)
    nb = N * np.random.choice([0.5, 0.625, 0.75, 0.875], BS)
    wt = np.random.choice([0.25, 0.5, 0.75, 1.0], (BS, 1, N))
    return {"X": bf(np.random.standard_normal((BS, NF, N)) * s[None, None, :] * c[None, :, None]),
            "W": bf(np.random.standard_normal((BS, N, N, J)) / np.sqrt(N) / s[None, None, :, None]),
            "N_batch": bf(nb),
            "mask": bf(wt),
            "cv1_w": bf(np.random.standard_normal((NOUT, KC)) / np.sqrt(KC) / t[None, :]),
            "cv1_b": bf(np.random.standard_normal(NOUT) * 0.5),
            "cv2_w": bf(np.random.standard_normal((NOUT, KC)) / np.sqrt(KC) / t[None, :]),
            "cv2_b": bf(np.random.standard_normal(NOUT) * 0.5),
            "bn_gamma": bf(1.0 + 0.1 * np.random.standard_normal(NOUT + NOUT)),
            "bn_beta": bf(0.3 * np.random.standard_normal(NOUT + NOUT))}


def reference(X, W, N_batch, mask, cv1_w, cv1_b, cv2_w, cv2_b, bn_gamma, bn_beta):
    mk = f64(mask)
    Xq = mxq(f64(X), 2, "e4m3")
    Wq = mxq(f64(W), 2, "e4m3")
    g = Wq.transpose(0, 3, 1, 2) @ Xq.transpose(0, 2, 1)[:, None]
    x1 = g.transpose(0, 1, 3, 2).reshape(BS, KC, N)
    x1q = mxq(x1, 1, "e4m3")
    y1 = (mxq(f64(cv1_w), 1, "e4m3") @ x1q) + f64(cv1_b)[None, :, None]
    z1 = np.maximum(y1, 0.0)
    yl1 = np.maximum((mxq(f64(cv2_w), 1, "e4m3") @ x1q) + f64(cv2_b)[None, :, None], 0.0)
    zb = np.concatenate([yl1, z1], axis=1)
    total = f64(N_batch).sum()
    mean = (zb * mk).sum(axis=(0, 2)) / total
    cz = zb - mean[None, :, None]
    var = (mk * cz * cz).sum(axis=(0, 2)) / total
    zbn = cz * (1.0 / np.sqrt(var + EPS))[None, :, None]
    return (f64(bn_gamma)[None, :, None] * zbn + f64(bn_beta)[None, :, None]) * mk

@@ -1,0 +1,392 @@
+from contextlib import ExitStack
+
+import concourse.mybir as mybir
+from concourse.masks import make_identity
+
+F32 = mybir.dt.float32
+BF16 = mybir.dt.bfloat16
+U32 = mybir.dt.uint32
+U8 = mybir.dt.uint8
+FP8X4 = mybir.dt.float8_e4m3fn_x4
+ALU = mybir.AluOpType
+ACT = mybir.ActivationFunctionType
+AXIS_X = mybir.AxisListType.X
+
+P = 128
+PACK = 4
+GRAPHS = 8
+FEATURES = 512
+NODES = 512
+OPERATORS = 3
+UNITS = GRAPHS * OPERATORS
+CONVS = 2
+CHANNELS = OPERATORS * FEATURES
+EPS = 1e-5
+
+TILES = 4
+PAIRS = 2
+PAIR_COLS = 2 * P
+
+SORT_AHEAD = 1
+QUANTISE_W_LAG = 1
+STEP_1_LAG = 2
+QUANTISE_X1_LAG = 3
+STEP_2_LAG = 4
+STATISTICS_LAG = 5
+
+FLOPS = 2 * GRAPHS * (OPERATORS * NODES * NODES * FEATURES + CONVS * P * CHANNELS * NODES)
+
+
+def tile_layer_simple_pa_t_kernel(
+    tc, X, W, N_batch, mask, cv1_w, cv1_b, cv2_w, cv2_b, bn_gamma, bn_beta, out
+):
+    nc = tc.nc
+    with ExitStack() as pools:
+        const = pools.enter_context(tc.tile_pool(name="const", bufs=1))
+        raw_pool = pools.enter_context(tc.tile_pool(name="raw", bufs=2))
+        unit_pool = pools.enter_context(tc.tile_pool(name="unit", bufs=3))
+        graph_pool = pools.enter_context(tc.tile_pool(name="graph", bufs=2))
+        stat_pool = pools.enter_context(tc.tile_pool(name="stat", bufs=4))
+        tr_psum = pools.enter_context(tc.psum_pool(name="tr_psum", bufs=3))
+        x1_psum = pools.enter_context(tc.psum_pool(name="x1_psum", bufs=3))
+        y_psum = pools.enter_context(tc.psum_pool(name="y_psum", bufs=CONVS))
+
+        w_raws, x_raws, x_groupeds, x_operands, y_banks = {}, {}, {}, {}, {}
+        w_sorteds, w_groupeds, w_operands, x1_groupeds, x1_operands = {}, {}, {}, {}, {}
+
+        def live(unit):
+            return 0 <= unit < UNITS
+
+        def load_operators(g):
+            if g >= GRAPHS:
+                return
+            w_raw = raw_pool.tile([P, TILES, NODES * OPERATORS], BF16)
+            nc.sync.dma_start(out=w_raw[:], in_=W[g].rearrange("(i p) n j -> p i (n j)", p=P))
+            w_raws[g] = w_raw
+
+        def load_features(g):
+            if g >= GRAPHS:
+                return
+            x_raw = raw_pool.tile([P, TILES, NODES], BF16)
+            nc.sync.dma_start(out=x_raw[:], in_=X[g].rearrange("(m t) n -> m t n", t=TILES))
+            x_raws[g] = x_raw
+
+        load_operators(0)
+        load_features(0)
+        cv_raws = []
+        for cv_w in (cv2_w, cv1_w):
+            cv_raw = const.tile([P, CHANNELS], BF16, name="cv_raw%d" % len(cv_raws))
+            nc.sync.dma_start(out=cv_raw[:], in_=cv_w)
+            cv_raws.append(cv_raw)
+        load_operators(1)
+        load_features(1)
+
+        mask_all = const.tile([P, GRAPHS, NODES], BF16)
+        nc.sync.dma_start(
+            out=mask_all[:].rearrange("p g m -> p (g m)"),
+            in_=mask.rearrange("g o m -> (g o m)").partition_broadcast(P),
+        )
+
+        ident_f32 = const.tile([P, P], F32)
+        make_identity(nc, ident_f32[:])
+        ident_bf16 = const.tile([P, P], BF16)
+        make_identity(nc, ident_bf16[:])
+        ones_f32 = const.tile([P, P], F32)
+        nc.vector.memset(ones_f32[:], 1.0)
+        eps = const.tile([P, 1], F32)
+        nc.vector.memset(eps[:], EPS)
+
+        warm = const.tile([P, 1], F32)
+        nc.scalar.activation(out=warm[:], in_=eps[:], func=ACT.Sqrt)
+
+        vector_rows = const.tile([P, P], BF16)
+        nc.vector.memset(vector_rows[:], 0.0)
+        nc.scalar.dma_start(out=vector_rows[0:1, :], in_=cv2_b.unsqueeze(0))
+        nc.scalar.dma_start(out=vector_rows[1:2, :], in_=cv1_b.unsqueeze(0))
+        nc.scalar.dma_start(out=vector_rows[2:4, :], in_=bn_gamma.rearrange("(h c) -> h c", h=CONVS))
+        nc.scalar.dma_start(out=vector_rows[4:6, :], in_=bn_beta.rearrange("(h c) -> h c", h=CONVS))
+        per_channel = const.tile([P, 3 * CONVS], F32)
+        bias = per_channel[:, 0:CONVS]
+        gamma = per_channel[:, CONVS : 2 * CONVS]
+        beta = per_channel[:, 2 * CONVS : 3 * CONVS]
+
+        mask_part = const.tile([P, GRAPHS * NODES // P], BF16)
+        nc.scalar.dma_start(
+            out=mask_part[:], in_=mask.rearrange("g o (q r) -> (g o q) r", r=GRAPHS * NODES // P)
+        )
+        counts_row = const.tile([P, GRAPHS], BF16)
+        nc.vector.memset(counts_row[:], 0.0)
+        nc.scalar.dma_start(out=counts_row[0:1, :], in_=N_batch.unsqueeze(0))
+
+        pivot = const.tile([P, CONVS], F32)
+        inv_total = const.tile([P, 1], F32)
+        ratio_less_2 = const.tile([P, 1], F32)
+        offset_0 = const.tile([P, CONVS], F32)
+        twice_offset_0 = const.tile([P, CONVS], F32)
+
+        def prepare_channel_vectors():
+            vector_cols = tr_psum.tile([P, P], BF16, tag="tr")
+            nc.tensor.transpose(vector_cols[:], vector_rows[:], ident_bf16[:])
+            nc.vector.tensor_copy(out=per_channel[:], in_=vector_cols[:, 0 : 3 * CONVS])
+            nc.vector.tensor_scalar_max(out=pivot[:], in0=bias, scalar1=0.0)
+
+            partial = const.tile([P, 2], F32)
+            nc.vector.reduce_sum(out=partial[:, 0:1], in_=mask_part[:], axis=AXIS_X)
+            nc.vector.reduce_sum(out=partial[:, 1:2], in_=counts_row[:], axis=AXIS_X)
+            totals_psum = tr_psum.tile([P, 2], F32, tag="tr")
+            nc.tensor.matmul(out=totals_psum[:], lhsT=ones_f32[:], rhs=partial[:], start=True, stop=True)
+            totals = const.tile([P, 2], F32)
+            nc.vector.tensor_copy(out=totals[:], in_=totals_psum[:])
+
+            nc.vector.reciprocal(out=inv_total[:], in_=totals[:, 1:2])
+            ratio_less_1 = const.tile([P, 1], F32)
+            nc.vector.tensor_scalar(
+                out=ratio_less_1[:],
+                in0=totals[:, 0:1],
+                scalar1=inv_total[:],
+                scalar2=-1.0,
+                op0=ALU.mult,
+                op1=ALU.add,
+            )
+            nc.vector.tensor_scalar_add(out=ratio_less_2[:], in0=ratio_less_1[:], scalar1=-1.0)
+            nc.vector.tensor_scalar_mul(out=offset_0[:], in0=pivot[:], scalar1=ratio_less_1[:])
+            nc.vector.tensor_scalar_mul(out=twice_offset_0[:], in0=offset_0[:], scalar1=2.0)
+
+        z = const.tile([P, CONVS, GRAPHS, NODES], F32)
+        first_parts = const.tile([P, CONVS, GRAPHS], F32)
+        second_parts = const.tile([P, CONVS, GRAPHS], F32)
+
+        cv_grouped = const.tile([P, OPERATORS, PAIR_COLS, PACK], BF16, align_bytes=64)
+        cv_codes = const.tile([P, OPERATORS, PAIR_COLS], U32, align_bytes=64)
+        cv_scales = const.tile([P, OPERATORS, PAIR_COLS], U8, align_bytes=64)
+
+        def transpose_conv_weights():
+            for j in range(OPERATORS):
+                cv_t = tr_psum.tile([P, 2, PAIR_COLS], F32, tag="tr")
+                transpose_words(cv_t, lambda i: cv_raws[i][:, FEATURES * j : FEATURES * (j + 1)], stepped)
+                nc.scalar.copy(
+                    out=cv_grouped[:, j].rearrange("p o t -> p (o t)").bitcast(F32).rearrange("p (o u) -> p o u", u=2),
+                    in_=cv_t[:].rearrange("p u c -> p c u"),
+                )
+
+        def quantise_conv_weights():
+            for j in range(OPERATORS):
+                nc.vector.quantize_mx(
+                    out=cv_codes[:, j, :].bitcast(FP8X4),
+                    scales=cv_scales[:, j, :],
+                    in_=cv_grouped[:, j].rearrange("p o t -> p (o t)"),
+                )
+
+        def stepped(u):
+            return slice(u, 2 * P, 2)
+
+        def in_halves(u):
+            return slice(P * u, P * (u + 1))
+
+        def transpose_words(bank, rows_of, words_of):
+            for u in range(2):
+                for i in range(2):
+                    nc.tensor.transpose(
+                        bank[:, u, P * i : P * (i + 1)],
+                        rows_of(i).bitcast(F32)[:, words_of(u)],
+                        ident_f32[:],
+                    )
+
+        def sort_operator(unit):
+            if not live(unit):
+                return
+            g, j = divmod(unit, OPERATORS)
+            w_sorted = unit_pool.tile([P, TILES, NODES], BF16)
+            nc.vector.tensor_copy(
+                out=w_sorted[:].rearrange("p i (u q e) -> p i u q e", u=2, e=2),
+                in_=w_raws[g][:].rearrange("p i (q u e j) -> p i u q e j", u=2, e=2, j=OPERATORS)[:, :, :, :, :, j],
+            )
+            w_sorteds[unit] = w_sorted
+            if j == OPERATORS - 1:
+                load_operators(g + 2)
+
+        def transpose_features(unit):
+            g, j = divmod(unit, OPERATORS)
+            if not live(unit) or j != 0:
+                return
+            x_grouped = graph_pool.tile([P, FEATURES, PACK], BF16, align_bytes=64)
+            x_groupeds[g] = x_grouped
+            for pair in range(PAIRS):
+                x_t = tr_psum.tile([P, 2, PAIR_COLS], F32, tag="tr")
+                transpose_words(x_t, lambda i: x_raws[g][:, 2 * pair + i, :], stepped)
+                nc.vector.tensor_copy(
+                    out=x_grouped[:].bitcast(F32)[:, PAIR_COLS * pair : PAIR_COLS * (pair + 1), :],
+                    in_=x_t[:].rearrange("p u c -> p c u"),
+                )
+            load_features(g + 2)
+
+        def transpose_operator(unit):
+            if not live(unit):
+                return
+            w_grouped = unit_pool.tile([P, NODES, PACK], BF16, align_bytes=64)
+            w_groupeds[unit] = w_grouped
+            for pair in range(PAIRS):
+                w_t = tr_psum.tile([P, 2, PAIR_COLS], F32, tag="tr")
+                transpose_words(w_t, lambda i: w_sorteds[unit][:, 2 * pair + i, :], in_halves)
+                nc.scalar.copy(
+                    out=w_grouped[:].bitcast(F32)[:, PAIR_COLS * pair : PAIR_COLS * (pair + 1), :],
+                    in_=w_t[:].rearrange("p u c -> p c u"),
+                )
+
+        def quantise(grouped, pool, kind):
+            codes = pool.tile([P, NODES], U32, align_bytes=64, name=kind + "_codes")
+            scales = pool.tile([P, NODES], U8, align_bytes=64, name=kind + "_scales")
+            nc.vector.quantize_mx(
+                out=codes[:].bitcast(FP8X4), scales=scales[:], in_=grouped[:].rearrange("p c t -> p (c t)")
+            )
+            return codes, scales
+
+        def quantise_operator(unit):
+            if not live(unit):
+                return
+            g, j = divmod(unit, OPERATORS)
+            w_operands[unit] = quantise(w_groupeds[unit], unit_pool, "w")
+            if j == 0:
+                x_operands[g] = quantise(x_groupeds[g], graph_pool, "x")
+
+        def apply_operator(unit):
+            if not live(unit):
+                return
+            x_codes, x_scales = x_operands[unit // OPERATORS]
+            w_codes, w_scales = w_operands[unit]
+            x1_grouped = unit_pool.tile([P, NODES, PACK], BF16, align_bytes=64)
+            x1_groupeds[unit] = x1_grouped
+            for i in range(TILES):
+                m_cols = slice(P * i, P * (i + 1))
+                x1_bank = x1_psum.tile([P, PACK, P], F32)
+                for t in range(PACK):
+                    f_cols = slice(P * t, P * (t + 1))
+                    nc.tensor.matmul_mx(
+                        out=x1_bank[:, t, :],
+                        lhsT=x_codes[:, f_cols].bitcast(FP8X4),
+                        lhsT_scale=x_scales[:, f_cols],
+                        rhs=w_codes[:, m_cols].bitcast(FP8X4),
+                        rhs_scale=w_scales[:, m_cols],
+                        start=True,
+                        stop=True,
+                    )
+                nc.scalar.copy(out=x1_grouped[:, m_cols, :], in_=x1_bank[:].rearrange("p t m -> p m t"))
+
+        def quantise_x1(unit):
+            if live(unit):
+                x1_operands[unit] = quantise(x1_groupeds[unit], unit_pool, "x1")
+
+        def convolve(unit):
+            if not live(unit):
+                return
+            g, j = divmod(unit, OPERATORS)
+            x1_codes, x1_scales = x1_operands[unit]
+            for conv in range(CONVS):
+                if j == 0:
+                    y = y_psum.tile([P, NODES], F32)
+                    y_banks[g, conv] = y
+                nc.tensor.matmul_mx(
+                    out=y_banks[g, conv][:],
+                    lhsT=cv_codes[:, j, P * conv : P * (conv + 1)].bitcast(FP8X4),
+                    lhsT_scale=cv_scales[:, j, P * conv : P * (conv + 1)],
+                    rhs=x1_codes[:].bitcast(FP8X4),
+                    rhs_scale=x1_scales[:],
+                    start=(j == 0),
+                    stop=(j == OPERATORS - 1),
+                )
+            if j == OPERATORS - 1:
+                for conv in range(CONVS):
+                    nc.scalar.activation(
+                        out=z[:, conv, g, :],
+                        in_=y_banks[g, conv][:],
+                        func=ACT.Relu,
+                        bias=bias[:, conv : conv + 1],
+                    )
+
+        def add_to_statistics(unit):
+            g, j = divmod(unit, OPERATORS)
+            if not live(unit) or j != OPERATORS - 1:
+                return
+            weighted = []
+            for conv in range(CONVS):
+                masked = stat_pool.tile([P, NODES], F32)
+                nc.vector.scalar_tensor_tensor(
+                    out=masked[:],
+                    in0=z[:, conv, g, :],
+                    scalar=pivot[:, conv : conv + 1],
+                    in1=mask_all[:, g, :],
+                    op0=ALU.subtract,
+                    op1=ALU.mult,
+                    accum_out=first_parts[:, conv, g : g + 1],
+                )
+                weighted.append(masked)
+            for conv in range(CONVS):
+                squares = stat_pool.tile([P, NODES], F32)
+                nc.vector.scalar_tensor_tensor(
+                    out=squares[:],
+                    in0=z[:, conv, g, :],
+                    scalar=pivot[:, conv : conv + 1],
+                    in1=weighted[conv][:],
+                    op0=ALU.subtract,
+                    op1=ALU.mult,
+                    accum_out=second_parts[:, conv, g : g + 1],
+                )
+
+        for turn in range(-SORT_AHEAD, UNITS + STATISTICS_LAG + 1):
+            transpose_features(turn)
+            transpose_operator(turn)
+            if turn == 0:
+                transpose_conv_weights()
+            apply_operator(turn - STEP_1_LAG)
+            convolve(turn - STEP_2_LAG)
+            quantise_x1(turn - QUANTISE_X1_LAG)
+            quantise_operator(turn - QUANTISE_W_LAG)
+            if turn == 1:
+                quantise_conv_weights()
+                prepare_channel_vectors()
+            add_to_statistics(turn - STATISTICS_LAG)
+            sort_operator(turn + SORT_AHEAD)
+
+        first = const.tile([P, CONVS], F32)
+        nc.vector.reduce_sum(out=first[:], in_=first_parts[:], axis=AXIS_X)
+        second = const.tile([P, CONVS], F32)
+        nc.vector.reduce_sum(out=second[:], in_=second_parts[:], axis=AXIS_X)
+        offset = const.tile([P, CONVS], F32)
+        nc.vector.scalar_tensor_tensor(
+            out=offset[:], in0=first[:], scalar=inv_total[:], in1=offset_0[:], op0=ALU.mult, op1=ALU.add
+        )
+        inner = const.tile([P, CONVS], F32)
+        nc.vector.scalar_tensor_tensor(
+            out=inner[:], in0=offset[:], scalar=ratio_less_2[:], in1=twice_offset_0[:], op0=ALU.mult, op1=ALU.add
+        )
+        correction = const.tile([P, CONVS], F32)
+        nc.vector.tensor_mul(out=correction[:], in0=inner[:], in1=offset[:])
+        var = const.tile([P, CONVS], F32)
+        nc.vector.scalar_tensor_tensor(
+            out=var[:], in0=second[:], scalar=inv_total[:], in1=correction[:], op0=ALU.mult, op1=ALU.add
+        )
+        std = const.tile([P, CONVS], F32)
+        nc.scalar.activation(out=std[:], in_=var[:], func=ACT.Sqrt, bias=eps[:])
+        mean = const.tile([P, CONVS], F32)
+        nc.vector.tensor_add(out=mean[:], in0=offset[:], in1=pivot[:])
+        inv_std = const.tile([P, CONVS], F32)
+        nc.vector.reciprocal(out=inv_std[:], in_=std[:])
+        gain = const.tile([P, CONVS], F32)
+        nc.vector.tensor_mul(out=gain[:], in0=gamma, in1=inv_std[:])
+        mean_gain = const.tile([P, CONVS], F32)
+        nc.vector.tensor_mul(out=mean_gain[:], in0=mean[:], in1=gain[:])
+        shift = const.tile([P, CONVS], F32)
+        nc.vector.tensor_sub(out=shift[:], in0=beta, in1=mean_gain[:])
+
+        for g in range(GRAPHS):
+            for conv in range(CONVS):
+                piece = z[:, conv, g, :]
+                nc.scalar.activation(
+                    out=piece,
+                    in_=piece,
+                    func=ACT.Identity,
+                    scale=gain[:, conv : conv + 1],
+                    bias=shift[:, conv : conv + 1],
+                )
+                nc.vector.tensor_mul(out=piece, in0=piece, in1=mask_all[:, g, :])
+                nc.sync.dma_start(out=out[g, P * conv : P * (conv + 1), :], in_=piece)

@@ -180,9 +180,6 @@ def tile_layer_simple_pa_t_kernel(
         def stepped(u):
             return slice(u, 2 * P, 2)
 
-        def in_halves(u):
-            return slice(P * u, P * (u + 1))
-
         def transpose_words(bank, rows_of, words_of):
             for u in range(2):
                 for i in range(2):
@@ -198,8 +195,7 @@ def tile_layer_simple_pa_t_kernel(
             g, j = divmod(unit, OPERATORS)
             w_sorted = unit_pool.tile([P, TILES, NODES], BF16)
             nc.vector.tensor_copy(
-                out=w_sorted[:].rearrange("p i (u q e) -> p i u q e", u=2, e=2),
-                in_=w_raws[g][:].rearrange("p i (q u e j) -> p i u q e j", u=2, e=2, j=OPERATORS)[:, :, :, :, :, j],
+                out=w_sorted[:], in_=w_raws[g][:].rearrange("p i (n j) -> p i n j", j=OPERATORS)[:, :, :, j]
             )
             w_sorteds[unit] = w_sorted
             if j == OPERATORS - 1:
@@ -227,7 +223,7 @@ def tile_layer_simple_pa_t_kernel(
             w_groupeds[unit] = w_grouped
             for pair in range(PAIRS):
                 w_t = tr_psum.tile([P, 2, PAIR_COLS], F32, tag="tr")
-                transpose_words(w_t, lambda i: w_sorteds[unit][:, 2 * pair + i, :], in_halves)
+                transpose_words(w_t, lambda i: w_sorteds[unit][:, 2 * pair + i, :], stepped)
                 nc.scalar.copy(
                     out=w_grouped[:].bitcast(F32)[:, PAIR_COLS * pair : PAIR_COLS * (pair + 1), :],
                     in_=w_t[:].rearrange("p u c -> p c u"),

@@ -118,7 +118,7 @@ def tile_layer_simple_pa_t_kernel(
         nc.vector.memset(counts_row[:], 0.0)
         nc.scalar.dma_start(out=counts_row[0:1, :], in_=N_batch.unsqueeze(0))
 
-        pivot = const.tile([P, CONVS], F32)
+        neg_bias = const.tile([P, CONVS], F32)
         inv_total = const.tile([P, 1], F32)
         ratio_less_2 = const.tile([P, 1], F32)
         offset_0 = const.tile([P, CONVS], F32)
@@ -128,7 +128,7 @@ def tile_layer_simple_pa_t_kernel(
             vector_cols = tr_psum.tile([P, P], BF16, tag="tr")
             nc.tensor.transpose(vector_cols[:], vector_rows[:], ident_bf16[:])
             nc.vector.tensor_copy(out=per_channel[:], in_=vector_cols[:, 0 : 3 * CONVS])
-            nc.vector.tensor_scalar_max(out=pivot[:], in0=bias, scalar1=0.0)
+            nc.vector.tensor_scalar_mul(out=neg_bias[:], in0=bias, scalar1=-1.0)
 
             partial = const.tile([P, 2], F32)
             nc.vector.reduce_sum(out=partial[:, 0:1], in_=mask_part[:], axis=AXIS_X)
@@ -149,10 +149,10 @@ def tile_layer_simple_pa_t_kernel(
                 op1=ALU.add,
             )
             nc.vector.tensor_scalar_add(out=ratio_less_2[:], in0=ratio_less_1[:], scalar1=-1.0)
-            nc.vector.tensor_scalar_mul(out=offset_0[:], in0=pivot[:], scalar1=ratio_less_1[:])
+            nc.vector.tensor_scalar_mul(out=offset_0[:], in0=bias, scalar1=ratio_less_1[:])
             nc.vector.tensor_scalar_mul(out=twice_offset_0[:], in0=offset_0[:], scalar1=2.0)
 
-        z = const.tile([P, CONVS, GRAPHS, NODES], F32)
+        zm = const.tile([P, CONVS, GRAPHS, NODES], F32)
         first_parts = const.tile([P, CONVS, GRAPHS], F32)
         second_parts = const.tile([P, CONVS, GRAPHS], F32)
 
@@ -210,7 +210,7 @@ def tile_layer_simple_pa_t_kernel(
             for pair in range(PAIRS):
                 x_t = tr_psum.tile([P, 2, PAIR_COLS], F32, tag="tr")
                 transpose_words(x_t, lambda i: x_raws[g][:, 2 * pair + i, :], stepped)
-                nc.vector.tensor_copy(
+                nc.scalar.copy(
                     out=x_grouped[:].bitcast(F32)[:, PAIR_COLS * pair : PAIR_COLS * (pair + 1), :],
                     in_=x_t[:].rearrange("p u c -> p c u"),
                 )
@@ -290,45 +290,35 @@ def tile_layer_simple_pa_t_kernel(
                     start=(j == 0),
                     stop=(j == OPERATORS - 1),
                 )
-            if j == OPERATORS - 1:
-                for conv in range(CONVS):
-                    nc.scalar.activation(
-                        out=z[:, conv, g, :],
-                        in_=y_banks[g, conv][:],
-                        func=ACT.Relu,
-                        bias=bias[:, conv : conv + 1],
-                    )
 
         def add_to_statistics(unit):
             g, j = divmod(unit, OPERATORS)
             if not live(unit) or j != OPERATORS - 1:
                 return
-            weighted = []
             for conv in range(CONVS):
-                masked = stat_pool.tile([P, NODES], F32)
                 nc.vector.scalar_tensor_tensor(
-                    out=masked[:],
-                    in0=z[:, conv, g, :],
-                    scalar=pivot[:, conv : conv + 1],
+                    out=zm[:, conv, g, :],
+                    in0=y_banks[g, conv][:],
+                    scalar=neg_bias[:, conv : conv + 1],
                     in1=mask_all[:, g, :],
-                    op0=ALU.subtract,
+                    op0=ALU.max,
                     op1=ALU.mult,
                     accum_out=first_parts[:, conv, g : g + 1],
                 )
-                weighted.append(masked)
             for conv in range(CONVS):
                 squares = stat_pool.tile([P, NODES], F32)
                 nc.vector.scalar_tensor_tensor(
                     out=squares[:],
-                    in0=z[:, conv, g, :],
-                    scalar=pivot[:, conv : conv + 1],
-                    in1=weighted[conv][:],
-                    op0=ALU.subtract,
+                    in0=y_banks[g, conv][:],
+                    scalar=neg_bias[:, conv : conv + 1],
+                    in1=zm[:, conv, g, :],
+                    op0=ALU.max,
                     op1=ALU.mult,
                     accum_out=second_parts[:, conv, g : g + 1],
                 )
 
         for turn in range(-SORT_AHEAD, UNITS + STATISTICS_LAG + 1):
+            add_to_statistics(turn - STATISTICS_LAG)
             transpose_features(turn)
             transpose_operator(turn)
             if turn == 0:
@@ -340,7 +330,6 @@ def tile_layer_simple_pa_t_kernel(
             if turn == 1:
                 quantise_conv_weights()
                 prepare_channel_vectors()
-            add_to_statistics(turn - STATISTICS_LAG)
             sort_operator(turn + SORT_AHEAD)
 
         first = const.tile([P, CONVS], F32)
@@ -361,28 +350,31 @@ def tile_layer_simple_pa_t_kernel(
         nc.vector.scalar_tensor_tensor(
             out=var[:], in0=second[:], scalar=inv_total[:], in1=correction[:], op0=ALU.mult, op1=ALU.add
         )
+        nc.vector.tensor_scalar_max(out=var[:], in0=var[:], scalar1=0.0)
         std = const.tile([P, CONVS], F32)
         nc.scalar.activation(out=std[:], in_=var[:], func=ACT.Sqrt, bias=eps[:])
-        mean = const.tile([P, CONVS], F32)
-        nc.vector.tensor_add(out=mean[:], in0=offset[:], in1=pivot[:])
         inv_std = const.tile([P, CONVS], F32)
         nc.vector.reciprocal(out=inv_std[:], in_=std[:])
         gain = const.tile([P, CONVS], F32)
         nc.vector.tensor_mul(out=gain[:], in0=gamma, in1=inv_std[:])
-        mean_gain = const.tile([P, CONVS], F32)
-        nc.vector.tensor_mul(out=mean_gain[:], in0=mean[:], in1=gain[:])
+        offset_gain = const.tile([P, CONVS], F32)
+        nc.vector.tensor_mul(out=offset_gain[:], in0=offset[:], in1=gain[:])
         shift = const.tile([P, CONVS], F32)
-        nc.vector.tensor_sub(out=shift[:], in0=beta, in1=mean_gain[:])
+        nc.vector.tensor_sub(out=shift[:], in0=beta, in1=offset_gain[:])
 
         for g in range(GRAPHS):
             for conv in range(CONVS):
-                piece = z[:, conv, g, :]
+                piece = zm[:, conv, g, :]
+                shifted = stat_pool.tile([P, NODES], F32)
                 nc.scalar.activation(
-                    out=piece,
-                    in_=piece,
-                    func=ACT.Identity,
-                    scale=gain[:, conv : conv + 1],
-                    bias=shift[:, conv : conv + 1],
+                    out=shifted[:], in_=mask_all[:, g, :], func=ACT.Copy, scale=shift[:, conv : conv + 1]
                 )
-                nc.vector.tensor_mul(out=piece, in0=piece, in1=mask_all[:, g, :])
+                nc.vector.scalar_tensor_tensor(
+                    out=piece,
+                    in0=piece,
+                    scalar=gain[:, conv : conv + 1],
+                    in1=shifted[:],
+                    op0=ALU.mult,
+                    op1=ALU.add,
+                )
                 nc.sync.dma_start(out=out[g, P * conv : P * (conv + 1), :], in_=piece)

@@ -54,14 +54,23 @@ def tile_layer_simple_pa_t_kernel(
         w_raws, x_raws, x_groupeds, x_operands, y_banks = {}, {}, {}, {}, {}
         w_sorteds, w_groupeds, w_operands, x1_groupeds, x1_operands = {}, {}, {}, {}, {}
 
+        def node_pieces(g):
+            half = NODES // 2
+            return [slice(0, half), slice(half, NODES)] if g == GRAPHS - 1 else [slice(0, NODES)]
+
         def live(unit):
             return 0 <= unit < UNITS
+
+        def pieces_of(g):
+            return [slice(0, 2), slice(2, TILES)] if g == 0 else [slice(0, TILES)]
 
         def load_operators(g):
             if g >= GRAPHS:
                 return
             w_raw = raw_pool.tile([P, TILES, NODES * OPERATORS], BF16)
-            nc.sync.dma_start(out=w_raw[:], in_=W[g].rearrange("(i p) n j -> p i (n j)", p=P))
+            rows = W[g].rearrange("(i p) n j -> p i (n j)", p=P)
+            for tiles in pieces_of(g):
+                nc.sync.dma_start(out=w_raw[:, tiles, :], in_=rows[:, tiles, :])
             w_raws[g] = w_raw
 
         def load_features(g):
@@ -71,8 +80,8 @@ def tile_layer_simple_pa_t_kernel(
             nc.sync.dma_start(out=x_raw[:], in_=X[g].rearrange("(m t) n -> m t n", t=TILES))
             x_raws[g] = x_raw
 
-        load_operators(0)
         load_features(0)
+        load_operators(0)
         cv_raws = []
         for cv_w in (cv2_w, cv1_w):
             cv_raw = const.tile([P, CHANNELS], BF16, name="cv_raw%d" % len(cv_raws))
@@ -97,7 +106,7 @@ def tile_layer_simple_pa_t_kernel(
         nc.vector.memset(eps[:], EPS)
 
         warm = const.tile([P, 1], F32)
-        nc.scalar.activation(out=warm[:], in_=eps[:], func=ACT.Sqrt)
+        nc.scalar.activation(out=warm[:], in_=eps[:], func=ACT.Abs_reciprocal_sqrt)
 
         vector_rows = const.tile([P, P], BF16)
         nc.vector.memset(vector_rows[:], 0.0)
@@ -153,8 +162,7 @@ def tile_layer_simple_pa_t_kernel(
             nc.vector.tensor_scalar_mul(out=twice_offset_0[:], in0=offset_0[:], scalar1=2.0)
 
         zm = const.tile([P, CONVS, GRAPHS, NODES], F32)
-        first_parts = const.tile([P, CONVS, GRAPHS], F32)
-        second_parts = const.tile([P, CONVS, GRAPHS], F32)
+        parts = const.tile([P, 2, CONVS, GRAPHS + 1], F32)
 
         cv_grouped = const.tile([P, OPERATORS, PAIR_COLS, PACK], BF16, align_bytes=64)
         cv_codes = const.tile([P, OPERATORS, PAIR_COLS], U32, align_bytes=64)
@@ -194,9 +202,9 @@ def tile_layer_simple_pa_t_kernel(
                 return
             g, j = divmod(unit, OPERATORS)
             w_sorted = unit_pool.tile([P, TILES, NODES], BF16)
-            nc.vector.tensor_copy(
-                out=w_sorted[:], in_=w_raws[g][:].rearrange("p i (n j) -> p i n j", j=OPERATORS)[:, :, :, j]
-            )
+            by_operator = w_raws[g][:].rearrange("p i (n j) -> p i n j", j=OPERATORS)
+            for tiles in pieces_of(g):
+                nc.vector.tensor_copy(out=w_sorted[:, tiles, :], in_=by_operator[:, tiles, :, j])
             w_sorteds[unit] = w_sorted
             if j == OPERATORS - 1:
                 load_operators(g + 2)
@@ -229,21 +237,27 @@ def tile_layer_simple_pa_t_kernel(
                     in_=w_t[:].rearrange("p u c -> p c u"),
                 )
 
-        def quantise(grouped, pool, kind):
+        def quantise(grouped, pool, kind, pieces=(slice(0, NODES),)):
             codes = pool.tile([P, NODES], U32, align_bytes=64, name=kind + "_codes")
             scales = pool.tile([P, NODES], U8, align_bytes=64, name=kind + "_scales")
-            nc.vector.quantize_mx(
-                out=codes[:].bitcast(FP8X4), scales=scales[:], in_=grouped[:].rearrange("p c t -> p (c t)")
-            )
+            for cols in pieces:
+                nc.vector.quantize_mx(
+                    out=codes[:, cols].bitcast(FP8X4),
+                    scales=scales[:, cols],
+                    in_=grouped[:, cols, :].rearrange("p c t -> p (c t)"),
+                )
             return codes, scales
+
+        def quantise_features(g):
+            x_operands[g] = quantise(x_groupeds[g], graph_pool, "x")
 
         def quantise_operator(unit):
             if not live(unit):
                 return
             g, j = divmod(unit, OPERATORS)
             w_operands[unit] = quantise(w_groupeds[unit], unit_pool, "w")
-            if j == 0:
-                x_operands[g] = quantise(x_groupeds[g], graph_pool, "x")
+            if j == 0 and g > 0:
+                quantise_features(g)
 
         def apply_operator(unit):
             if not live(unit):
@@ -266,115 +280,143 @@ def tile_layer_simple_pa_t_kernel(
                         start=True,
                         stop=True,
                     )
-                nc.scalar.copy(out=x1_grouped[:, m_cols, :], in_=x1_bank[:].rearrange("p t m -> p m t"))
+                copy = nc.vector.tensor_copy if unit >= UNITS - 2 and i % 2 else nc.scalar.copy
+                copy(out=x1_grouped[:, m_cols, :], in_=x1_bank[:].rearrange("p t m -> p m t"))
 
         def quantise_x1(unit):
             if live(unit):
-                x1_operands[unit] = quantise(x1_groupeds[unit], unit_pool, "x1")
+                pieces = node_pieces(unit // OPERATORS) if unit == UNITS - 1 else [slice(0, NODES)]
+                x1_operands[unit] = quantise(x1_groupeds[unit], unit_pool, "x1", pieces)
 
         def convolve(unit):
             if not live(unit):
                 return
             g, j = divmod(unit, OPERATORS)
             x1_codes, x1_scales = x1_operands[unit]
-            for conv in range(CONVS):
-                if j == 0:
-                    y = y_psum.tile([P, NODES], F32)
-                    y_banks[g, conv] = y
-                nc.tensor.matmul_mx(
-                    out=y_banks[g, conv][:],
-                    lhsT=cv_codes[:, j, P * conv : P * (conv + 1)].bitcast(FP8X4),
-                    lhsT_scale=cv_scales[:, j, P * conv : P * (conv + 1)],
-                    rhs=x1_codes[:].bitcast(FP8X4),
-                    rhs_scale=x1_scales[:],
-                    start=(j == 0),
-                    stop=(j == OPERATORS - 1),
-                )
+            for piece, cols in enumerate(node_pieces(g)):
+                for conv in range(CONVS):
+                    if j == 0:
+                        if piece == 0:
+                            y = y_psum.tile([P, NODES], F32, tag="y")
+                        else:
+                            y = tr_psum.tile([P, NODES], F32, tag="tr")
+                        y_banks[g, conv, piece] = y[:, 0 : cols.stop - cols.start]
+                    nc.tensor.matmul_mx(
+                        out=y_banks[g, conv, piece],
+                        lhsT=cv_codes[:, j, P * conv : P * (conv + 1)].bitcast(FP8X4),
+                        lhsT_scale=cv_scales[:, j, P * conv : P * (conv + 1)],
+                        rhs=x1_codes[:, cols].bitcast(FP8X4),
+                        rhs_scale=x1_scales[:, cols],
+                        start=(j == 0),
+                        stop=(j == OPERATORS - 1),
+                    )
 
         def add_to_statistics(unit):
             g, j = divmod(unit, OPERATORS)
             if not live(unit) or j != OPERATORS - 1:
                 return
-            for conv in range(CONVS):
-                nc.vector.scalar_tensor_tensor(
-                    out=zm[:, conv, g, :],
-                    in0=y_banks[g, conv][:],
-                    scalar=neg_bias[:, conv : conv + 1],
-                    in1=mask_all[:, g, :],
-                    op0=ALU.max,
-                    op1=ALU.mult,
-                    accum_out=first_parts[:, conv, g : g + 1],
-                )
-            for conv in range(CONVS):
-                squares = stat_pool.tile([P, NODES], F32)
-                nc.vector.scalar_tensor_tensor(
-                    out=squares[:],
-                    in0=y_banks[g, conv][:],
-                    scalar=neg_bias[:, conv : conv + 1],
-                    in1=zm[:, conv, g, :],
-                    op0=ALU.max,
-                    op1=ALU.mult,
-                    accum_out=second_parts[:, conv, g : g + 1],
-                )
+            for piece, cols in enumerate(node_pieces(g)):
+                part = g + piece
+                for conv in range(CONVS):
+                    nc.vector.scalar_tensor_tensor(
+                        out=zm[:, conv, g, cols],
+                        in0=y_banks[g, conv, piece],
+                        scalar=neg_bias[:, conv : conv + 1],
+                        in1=mask_all[:, g, cols],
+                        op0=ALU.max,
+                        op1=ALU.mult,
+                        accum_out=parts[:, 0, conv, part : part + 1],
+                    )
+                for conv in range(CONVS):
+                    squares = stat_pool.tile([P, NODES], F32)
+                    nc.vector.scalar_tensor_tensor(
+                        out=squares[:, cols],
+                        in0=y_banks[g, conv, piece],
+                        scalar=neg_bias[:, conv : conv + 1],
+                        in1=zm[:, conv, g, cols],
+                        op0=ALU.max,
+                        op1=ALU.mult,
+                        accum_out=parts[:, 1, conv, part : part + 1],
+                    )
 
         for turn in range(-SORT_AHEAD, UNITS + STATISTICS_LAG + 1):
             add_to_statistics(turn - STATISTICS_LAG)
             transpose_features(turn)
             transpose_operator(turn)
-            if turn == 0:
+            if turn == 1:
                 transpose_conv_weights()
             apply_operator(turn - STEP_1_LAG)
             convolve(turn - STEP_2_LAG)
             quantise_x1(turn - QUANTISE_X1_LAG)
             quantise_operator(turn - QUANTISE_W_LAG)
-            if turn == 1:
+            if turn == 0:
+                quantise_features(0)
+            if turn == 3:
                 quantise_conv_weights()
                 prepare_channel_vectors()
             sort_operator(turn + SORT_AHEAD)
 
-        first = const.tile([P, CONVS], F32)
-        nc.vector.reduce_sum(out=first[:], in_=first_parts[:], axis=AXIS_X)
-        second = const.tile([P, CONVS], F32)
-        nc.vector.reduce_sum(out=second[:], in_=second_parts[:], axis=AXIS_X)
+        sums = const.tile([P, 2 * CONVS], F32)
+        nc.vector.reduce_sum(out=sums[:], in_=parts[:].rearrange("p s c k -> p (s c) k"), axis=AXIS_X)
+        first, second = sums[:, 0:CONVS], sums[:, CONVS : 2 * CONVS]
         offset = const.tile([P, CONVS], F32)
         nc.vector.scalar_tensor_tensor(
-            out=offset[:], in0=first[:], scalar=inv_total[:], in1=offset_0[:], op0=ALU.mult, op1=ALU.add
+            out=offset[:], in0=first, scalar=inv_total[:], in1=offset_0[:], op0=ALU.mult, op1=ALU.add
         )
+        mean_square = const.tile([P, CONVS], F32)
+        nc.vector.tensor_scalar_mul(out=mean_square[:], in0=second, scalar1=inv_total[:])
         inner = const.tile([P, CONVS], F32)
         nc.vector.scalar_tensor_tensor(
             out=inner[:], in0=offset[:], scalar=ratio_less_2[:], in1=twice_offset_0[:], op0=ALU.mult, op1=ALU.add
         )
-        correction = const.tile([P, CONVS], F32)
-        nc.vector.tensor_mul(out=correction[:], in0=inner[:], in1=offset[:])
+        neg_offset = const.tile([P, CONVS], F32)
+        nc.vector.tensor_scalar_mul(out=neg_offset[:], in0=offset[:], scalar1=-1.0)
         var = const.tile([P, CONVS], F32)
-        nc.vector.scalar_tensor_tensor(
-            out=var[:], in0=second[:], scalar=inv_total[:], in1=correction[:], op0=ALU.mult, op1=ALU.add
-        )
-        nc.vector.tensor_scalar_max(out=var[:], in0=var[:], scalar1=0.0)
-        std = const.tile([P, CONVS], F32)
-        nc.scalar.activation(out=std[:], in_=var[:], func=ACT.Sqrt, bias=eps[:])
+        for conv in range(CONVS):
+            column = slice(conv, conv + 1)
+            nc.vector.scalar_tensor_tensor(
+                out=var[:, column],
+                in0=inner[:, column],
+                scalar=offset[:, column],
+                in1=mean_square[:, column],
+                op0=ALU.mult,
+                op1=ALU.add,
+            )
         inv_std = const.tile([P, CONVS], F32)
-        nc.vector.reciprocal(out=inv_std[:], in_=std[:])
+        nc.scalar.activation(out=inv_std[:], in_=var[:], func=ACT.Abs_reciprocal_sqrt, bias=eps[:])
         gain = const.tile([P, CONVS], F32)
-        nc.vector.tensor_mul(out=gain[:], in0=gamma, in1=inv_std[:])
-        offset_gain = const.tile([P, CONVS], F32)
-        nc.vector.tensor_mul(out=offset_gain[:], in0=offset[:], in1=gain[:])
+        for conv in range(CONVS):
+            column = slice(conv, conv + 1)
+            nc.scalar.activation(
+                out=gain[:, column], in_=inv_std[:, column], func=ACT.Copy, scale=gamma[:, column]
+            )
         shift = const.tile([P, CONVS], F32)
-        nc.vector.tensor_sub(out=shift[:], in0=beta, in1=offset_gain[:])
+        for conv in range(CONVS):
+            column = slice(conv, conv + 1)
+            nc.scalar.activation(
+                out=shift[:, column],
+                in_=gain[:, column],
+                func=ACT.Identity,
+                scale=neg_offset[:, column],
+                bias=beta[:, column],
+            )
 
         for g in range(GRAPHS):
             for conv in range(CONVS):
-                piece = zm[:, conv, g, :]
-                shifted = stat_pool.tile([P, NODES], F32)
-                nc.scalar.activation(
-                    out=shifted[:], in_=mask_all[:, g, :], func=ACT.Copy, scale=shift[:, conv : conv + 1]
-                )
-                nc.vector.scalar_tensor_tensor(
-                    out=piece,
-                    in0=piece,
-                    scalar=gain[:, conv : conv + 1],
-                    in1=shifted[:],
-                    op0=ALU.mult,
-                    op1=ALU.add,
-                )
-                nc.sync.dma_start(out=out[g, P * conv : P * (conv + 1), :], in_=piece)
+                half = NODES // 2
+                whole = [slice(0, NODES)]
+                for cols in [slice(0, half), slice(half, NODES)] if g == conv == 0 else whole:
+                    piece = zm[:, conv, g, cols]
+                    shifted = stat_pool.tile([P, NODES], F32)
+                    nc.scalar.activation(
+                        out=shifted[:, cols], in_=mask_all[:, g, cols], func=ACT.Copy, scale=shift[:, conv : conv + 1]
+                    )
+                    nc.vector.scalar_tensor_tensor(
+                        out=piece,
+                        in0=piece,
+                        scalar=gain[:, conv : conv + 1],
+                        in1=shifted[:, cols],
+                        op0=ALU.mult,
+                        op1=ALU.add,
+                    )
+                    nc.sync.dma_start(out=out[g, P * conv : P * (conv + 1), cols], in_=piece)

@@ -26,6 +26,7 @@ EPS = 1e-5
 TILES = 4
 PAIRS = 2
 PAIR_COLS = 2 * P
+RUN = 16
 
 SORT_AHEAD = 1
 QUANTISE_W_LAG = 1
@@ -188,6 +189,9 @@ def tile_layer_simple_pa_t_kernel(
         def stepped(u):
             return slice(u, 2 * P, 2)
 
+        def in_halves(u):
+            return slice(P * u, P * (u + 1))
+
         def transpose_words(bank, rows_of, words_of):
             for u in range(2):
                 for i in range(2):
@@ -202,9 +206,10 @@ def tile_layer_simple_pa_t_kernel(
                 return
             g, j = divmod(unit, OPERATORS)
             w_sorted = unit_pool.tile([P, TILES, NODES], BF16)
-            by_operator = w_raws[g][:].rearrange("p i (n j) -> p i n j", j=OPERATORS)
+            by_operator = w_raws[g][:].rearrange("p i (q u c j) -> p i u q c j", u=2, c=RUN, j=OPERATORS)
+            by_half = w_sorted[:].rearrange("p i (u q c) -> p i u q c", u=2, c=RUN)
             for tiles in pieces_of(g):
-                nc.vector.tensor_copy(out=w_sorted[:, tiles, :], in_=by_operator[:, tiles, :, j])
+                nc.vector.tensor_copy(out=by_half[:, tiles], in_=by_operator[:, tiles, :, :, :, j])
             w_sorteds[unit] = w_sorted
             if j == OPERATORS - 1:
                 load_operators(g + 2)
@@ -213,11 +218,16 @@ def tile_layer_simple_pa_t_kernel(
             g, j = divmod(unit, OPERATORS)
             if not live(unit) or j != 0:
                 return
+            x_sorted = graph_pool.tile([P, TILES, NODES], BF16)
+            nc.vector.tensor_copy(
+                out=x_sorted[:].rearrange("p i (u q c) -> p i u q c", u=2, c=RUN),
+                in_=x_raws[g][:].rearrange("p i (q u c) -> p i u q c", u=2, c=RUN),
+            )
             x_grouped = graph_pool.tile([P, FEATURES, PACK], BF16, align_bytes=64)
             x_groupeds[g] = x_grouped
             for pair in range(PAIRS):
                 x_t = tr_psum.tile([P, 2, PAIR_COLS], F32, tag="tr")
-                transpose_words(x_t, lambda i: x_raws[g][:, 2 * pair + i, :], stepped)
+                transpose_words(x_t, lambda i: x_sorted[:, 2 * pair + i, :], in_halves)
                 nc.scalar.copy(
                     out=x_grouped[:].bitcast(F32)[:, PAIR_COLS * pair : PAIR_COLS * (pair + 1), :],
                     in_=x_t[:].rearrange("p u c -> p c u"),
@@ -231,7 +241,7 @@ def tile_layer_simple_pa_t_kernel(
             w_groupeds[unit] = w_grouped
             for pair in range(PAIRS):
                 w_t = tr_psum.tile([P, 2, PAIR_COLS], F32, tag="tr")
-                transpose_words(w_t, lambda i: w_sorteds[unit][:, 2 * pair + i, :], stepped)
+                transpose_words(w_t, lambda i: w_sorteds[unit][:, 2 * pair + i, :], in_halves)
                 nc.scalar.copy(
                     out=w_grouped[:].bitcast(F32)[:, PAIR_COLS * pair : PAIR_COLS * (pair + 1), :],
                     in_=w_t[:].rearrange("p u c -> p c u"),

@@ -34,6 +34,8 @@ STEP_1_LAG = 2
 QUANTISE_X1_LAG = 3
 STEP_2_LAG = 4
 STATISTICS_LAG = 5
+CONV_WEIGHTS_TURN = 1
+PREPARATION_TURN = 2
 
 FLOPS = 2 * GRAPHS * (OPERATORS * NODES * NODES * FEATURES + CONVS * P * CHANNELS * NODES)
 
@@ -46,13 +48,13 @@ def tile_layer_simple_pa_t_kernel(
         const = pools.enter_context(tc.tile_pool(name="const", bufs=1))
         raw_pool = pools.enter_context(tc.tile_pool(name="raw", bufs=2))
         unit_pool = pools.enter_context(tc.tile_pool(name="unit", bufs=3))
+        x1_pool = pools.enter_context(tc.tile_pool(name="x1", bufs=2 * OPERATORS))
         graph_pool = pools.enter_context(tc.tile_pool(name="graph", bufs=2))
         stat_pool = pools.enter_context(tc.tile_pool(name="stat", bufs=4))
-        tr_psum = pools.enter_context(tc.psum_pool(name="tr_psum", bufs=3))
-        x1_psum = pools.enter_context(tc.psum_pool(name="x1_psum", bufs=3))
+        bank_psum = pools.enter_context(tc.psum_pool(name="bank_psum", bufs=6))
         y_psum = pools.enter_context(tc.psum_pool(name="y_psum", bufs=CONVS))
 
-        w_raws, x_raws, x_groupeds, x_operands, y_banks = {}, {}, {}, {}, {}
+        w_raws, x_raws, x_sorteds, x_groupeds, x_operands, y_banks = {}, {}, {}, {}, {}, {}
         w_sorteds, w_groupeds, w_operands, x1_groupeds, x1_operands = {}, {}, {}, {}, {}
 
         def node_pieces(g):
@@ -134,33 +136,43 @@ def tile_layer_simple_pa_t_kernel(
         offset_0 = const.tile([P, CONVS], F32)
         twice_offset_0 = const.tile([P, CONVS], F32)
 
-        def prepare_channel_vectors():
-            vector_cols = tr_psum.tile([P, P], BF16, tag="tr")
-            nc.tensor.transpose(vector_cols[:], vector_rows[:], ident_bf16[:])
-            nc.vector.tensor_copy(out=per_channel[:], in_=vector_cols[:, 0 : 3 * CONVS])
-            nc.vector.tensor_scalar_mul(out=neg_bias[:], in0=bias, scalar1=-1.0)
+        partial = const.tile([P, 2], F32)
+        totals = const.tile([P, 2], F32)
+        ratio_less_1 = const.tile([P, 1], F32)
+        preparation_banks = {}
 
-            partial = const.tile([P, 2], F32)
-            nc.vector.reduce_sum(out=partial[:, 0:1], in_=mask_part[:], axis=AXIS_X)
-            nc.vector.reduce_sum(out=partial[:, 1:2], in_=counts_row[:], axis=AXIS_X)
-            totals_psum = tr_psum.tile([P, 2], F32, tag="tr")
-            nc.tensor.matmul(out=totals_psum[:], lhsT=ones_f32[:], rhs=partial[:], start=True, stop=True)
-            totals = const.tile([P, 2], F32)
-            nc.vector.tensor_copy(out=totals[:], in_=totals_psum[:])
-
-            nc.vector.reciprocal(out=inv_total[:], in_=totals[:, 1:2])
-            ratio_less_1 = const.tile([P, 1], F32)
-            nc.vector.tensor_scalar(
-                out=ratio_less_1[:],
-                in0=totals[:, 0:1],
-                scalar1=inv_total[:],
-                scalar2=-1.0,
-                op0=ALU.mult,
-                op1=ALU.add,
-            )
-            nc.vector.tensor_scalar_add(out=ratio_less_2[:], in0=ratio_less_1[:], scalar1=-1.0)
-            nc.vector.tensor_scalar_mul(out=offset_0[:], in0=bias, scalar1=ratio_less_1[:])
-            nc.vector.tensor_scalar_mul(out=twice_offset_0[:], in0=offset_0[:], scalar1=2.0)
+        def prepare(step):
+            if step == 0:
+                vector_cols = bank_psum.tile([P, P], BF16, tag="bank")
+                nc.tensor.transpose(vector_cols[:], vector_rows[:], ident_bf16[:])
+                preparation_banks["vectors"] = vector_cols
+                nc.vector.reduce_sum(out=partial[:, 0:1], in_=mask_part[:], axis=AXIS_X)
+            elif step == 1:
+                nc.vector.tensor_copy(out=per_channel[:], in_=preparation_banks["vectors"][:, 0 : 3 * CONVS])
+                nc.vector.reduce_sum(out=partial[:, 1:2], in_=counts_row[:], axis=AXIS_X)
+            elif step == 2:
+                totals_psum = bank_psum.tile([P, 2], F32, tag="bank")
+                nc.tensor.matmul(out=totals_psum[:], lhsT=ones_f32[:], rhs=partial[:], start=True, stop=True)
+                preparation_banks["totals"] = totals_psum
+                nc.vector.tensor_scalar_mul(out=neg_bias[:], in0=bias, scalar1=-1.0)
+            elif step == 3:
+                nc.vector.tensor_copy(out=totals[:], in_=preparation_banks["totals"][:])
+            elif step == 4:
+                nc.vector.reciprocal(out=inv_total[:], in_=totals[:, 1:2])
+            elif step == 5:
+                nc.vector.tensor_scalar(
+                    out=ratio_less_1[:],
+                    in0=totals[:, 0:1],
+                    scalar1=inv_total[:],
+                    scalar2=-1.0,
+                    op0=ALU.mult,
+                    op1=ALU.add,
+                )
+            elif step == 6:
+                nc.vector.tensor_scalar_add(out=ratio_less_2[:], in0=ratio_less_1[:], scalar1=-1.0)
+                nc.vector.tensor_scalar_mul(out=offset_0[:], in0=bias, scalar1=ratio_less_1[:])
+            elif step == 7:
+                nc.vector.tensor_scalar_mul(out=twice_offset_0[:], in0=offset_0[:], scalar1=2.0)
 
         zm = const.tile([P, CONVS, GRAPHS, NODES], F32)
         parts = const.tile([P, 2, CONVS, GRAPHS + 1], F32)
@@ -171,7 +183,7 @@ def tile_layer_simple_pa_t_kernel(
 
         def transpose_conv_weights():
             for j in range(OPERATORS):
-                cv_t = tr_psum.tile([P, 2, PAIR_COLS], F32, tag="tr")
+                cv_t = bank_psum.tile([P, 2, PAIR_COLS], F32, tag="bank")
                 transpose_words(cv_t, lambda i: cv_raws[i][:, FEATURES * j : FEATURES * (j + 1)], stepped)
                 nc.scalar.copy(
                     out=cv_grouped[:, j].rearrange("p o t -> p (o t)").bitcast(F32).rearrange("p (o u) -> p o u", u=2),
@@ -214,25 +226,29 @@ def tile_layer_simple_pa_t_kernel(
             if j == OPERATORS - 1:
                 load_operators(g + 2)
 
-        def transpose_features(unit):
-            g, j = divmod(unit, OPERATORS)
-            if not live(unit) or j != 0:
+        def sort_features(g):
+            if g >= GRAPHS:
                 return
             x_sorted = graph_pool.tile([P, TILES, NODES], BF16)
             nc.vector.tensor_copy(
                 out=x_sorted[:].rearrange("p i (u q c) -> p i u q c", u=2, c=RUN),
                 in_=x_raws[g][:].rearrange("p i (q u c) -> p i u q c", u=2, c=RUN),
             )
+            x_sorteds[g] = x_sorted
+            load_features(g + 2)
+
+        def transpose_features(g):
+            if g >= GRAPHS:
+                return
             x_grouped = graph_pool.tile([P, FEATURES, PACK], BF16, align_bytes=64)
             x_groupeds[g] = x_grouped
             for pair in range(PAIRS):
-                x_t = tr_psum.tile([P, 2, PAIR_COLS], F32, tag="tr")
-                transpose_words(x_t, lambda i: x_sorted[:, 2 * pair + i, :], in_halves)
+                x_t = bank_psum.tile([P, 2, PAIR_COLS], F32, tag="bank")
+                transpose_words(x_t, lambda i: x_sorteds[g][:, 2 * pair + i, :], in_halves)
                 nc.scalar.copy(
                     out=x_grouped[:].bitcast(F32)[:, PAIR_COLS * pair : PAIR_COLS * (pair + 1), :],
                     in_=x_t[:].rearrange("p u c -> p c u"),
                 )
-            load_features(g + 2)
 
         def transpose_operator(unit):
             if not live(unit):
@@ -240,7 +256,7 @@ def tile_layer_simple_pa_t_kernel(
             w_grouped = unit_pool.tile([P, NODES, PACK], BF16, align_bytes=64)
             w_groupeds[unit] = w_grouped
             for pair in range(PAIRS):
-                w_t = tr_psum.tile([P, 2, PAIR_COLS], F32, tag="tr")
+                w_t = bank_psum.tile([P, 2, PAIR_COLS], F32, tag="bank")
                 transpose_words(w_t, lambda i: w_sorteds[unit][:, 2 * pair + i, :], in_halves)
                 nc.scalar.copy(
                     out=w_grouped[:].bitcast(F32)[:, PAIR_COLS * pair : PAIR_COLS * (pair + 1), :],
@@ -259,15 +275,12 @@ def tile_layer_simple_pa_t_kernel(
             return codes, scales
 
         def quantise_features(g):
-            x_operands[g] = quantise(x_groupeds[g], graph_pool, "x")
+            if g < GRAPHS:
+                x_operands[g] = quantise(x_groupeds[g], graph_pool, "x")
 
         def quantise_operator(unit):
-            if not live(unit):
-                return
-            g, j = divmod(unit, OPERATORS)
-            w_operands[unit] = quantise(w_groupeds[unit], unit_pool, "w")
-            if j == 0 and g > 0:
-                quantise_features(g)
+            if live(unit):
+                w_operands[unit] = quantise(w_groupeds[unit], unit_pool, "w")
 
         def apply_operator(unit):
             if not live(unit):
@@ -278,7 +291,7 @@ def tile_layer_simple_pa_t_kernel(
             x1_groupeds[unit] = x1_grouped
             for i in range(TILES):
                 m_cols = slice(P * i, P * (i + 1))
-                x1_bank = x1_psum.tile([P, PACK, P], F32)
+                x1_bank = bank_psum.tile([P, PACK, P], F32, tag="bank")
                 for t in range(PACK):
                     f_cols = slice(P * t, P * (t + 1))
                     nc.tensor.matmul_mx(
@@ -290,36 +303,39 @@ def tile_layer_simple_pa_t_kernel(
                         start=True,
                         stop=True,
                     )
-                copy = nc.vector.tensor_copy if unit >= UNITS - 2 and i % 2 else nc.scalar.copy
-                copy(out=x1_grouped[:, m_cols, :], in_=x1_bank[:].rearrange("p t m -> p m t"))
+                nc.scalar.copy(out=x1_grouped[:, m_cols, :], in_=x1_bank[:].rearrange("p t m -> p m t"))
 
         def quantise_x1(unit):
             if live(unit):
                 pieces = node_pieces(unit // OPERATORS) if unit == UNITS - 1 else [slice(0, NODES)]
-                x1_operands[unit] = quantise(x1_groupeds[unit], unit_pool, "x1", pieces)
+                x1_operands[unit] = quantise(x1_groupeds[unit], x1_pool, "x1", pieces)
 
         def convolve(unit):
             if not live(unit):
                 return
             g, j = divmod(unit, OPERATORS)
-            x1_codes, x1_scales = x1_operands[unit]
+            last = g == GRAPHS - 1
+            if j < OPERATORS - 1 and not last:
+                return
             for piece, cols in enumerate(node_pieces(g)):
                 for conv in range(CONVS):
-                    if j == 0:
+                    if (g, conv, piece) not in y_banks:
                         if piece == 0:
                             y = y_psum.tile([P, NODES], F32, tag="y")
                         else:
-                            y = tr_psum.tile([P, NODES], F32, tag="tr")
+                            y = bank_psum.tile([P, NODES], F32, tag="bank")
                         y_banks[g, conv, piece] = y[:, 0 : cols.stop - cols.start]
-                    nc.tensor.matmul_mx(
-                        out=y_banks[g, conv, piece],
-                        lhsT=cv_codes[:, j, P * conv : P * (conv + 1)].bitcast(FP8X4),
-                        lhsT_scale=cv_scales[:, j, P * conv : P * (conv + 1)],
-                        rhs=x1_codes[:, cols].bitcast(FP8X4),
-                        rhs_scale=x1_scales[:, cols],
-                        start=(j == 0),
-                        stop=(j == OPERATORS - 1),
-                    )
+                    for operator in [j] if last else range(OPERATORS):
+                        x1_codes, x1_scales = x1_operands[OPERATORS * g + operator]
+                        nc.tensor.matmul_mx(
+                            out=y_banks[g, conv, piece],
+                            lhsT=cv_codes[:, operator, P * conv : P * (conv + 1)].bitcast(FP8X4),
+                            lhsT_scale=cv_scales[:, operator, P * conv : P * (conv + 1)],
+                            rhs=x1_codes[:, cols].bitcast(FP8X4),
+                            rhs_scale=x1_scales[:, cols],
+                            start=(operator == 0),
+                            stop=(operator == OPERATORS - 1),
+                        )
 
         def add_to_statistics(unit):
             g, j = divmod(unit, OPERATORS)
@@ -349,22 +365,35 @@ def tile_layer_simple_pa_t_kernel(
                         accum_out=parts[:, 1, conv, part : part + 1],
                     )
 
-        for turn in range(-SORT_AHEAD, UNITS + STATISTICS_LAG + 1):
-            add_to_statistics(turn - STATISTICS_LAG)
-            transpose_features(turn)
-            transpose_operator(turn)
-            if turn == 1:
-                transpose_conv_weights()
-            apply_operator(turn - STEP_1_LAG)
-            convolve(turn - STEP_2_LAG)
-            quantise_x1(turn - QUANTISE_X1_LAG)
-            quantise_operator(turn - QUANTISE_W_LAG)
-            if turn == 0:
-                quantise_features(0)
-            if turn == 3:
-                quantise_conv_weights()
-                prepare_channel_vectors()
-            sort_operator(turn + SORT_AHEAD)
+        with tc.manual_schedule(
+            engines={mybir.EngineType.PE, mybir.EngineType.DVE, mybir.EngineType.Activation}
+        ):
+            sort_features(0)
+            sort_operator(0)
+            transpose_features(0)
+            transpose_operator(0)
+            quantise_features(0)
+            sort_operator(1)
+            for turn in range(1, UNITS + STATISTICS_LAG):
+                g, j = divmod(turn, OPERATORS)
+                sort_operator(turn + SORT_AHEAD)
+                quantise_operator(turn - QUANTISE_W_LAG)
+                if j == 1:
+                    sort_features(g + 1)
+                add_to_statistics(turn - STATISTICS_LAG)
+                apply_operator(turn - STEP_1_LAG)
+                quantise_x1(turn - QUANTISE_X1_LAG)
+                if j == 2:
+                    transpose_features(g + 1)
+                transpose_operator(turn)
+                convolve(turn - STEP_2_LAG)
+                if j == 0:
+                    quantise_features(g)
+                if turn == CONV_WEIGHTS_TURN:
+                    transpose_conv_weights()
+                if turn == CONV_WEIGHTS_TURN + 2:
+                    quantise_conv_weights()
+                prepare(turn - PREPARATION_TURN)
 
         sums = const.tile([P, 2 * CONVS], F32)
         nc.vector.reduce_sum(out=sums[:], in_=parts[:].rearrange("p s c k -> p (s c) k"), axis=AXIS_X)

@@ -245,7 +245,8 @@ def tile_layer_simple_pa_t_kernel(
             for pair in range(PAIRS):
                 x_t = bank_psum.tile([P, 2, PAIR_COLS], F32, tag="bank")
                 transpose_words(x_t, lambda i: x_sorteds[g][:, 2 * pair + i, :], in_halves)
-                nc.scalar.copy(
+                copy = nc.vector.tensor_copy if pair else nc.scalar.copy
+                copy(
                     out=x_grouped[:].bitcast(F32)[:, PAIR_COLS * pair : PAIR_COLS * (pair + 1), :],
                     in_=x_t[:].rearrange("p u c -> p c u"),
                 )
@@ -381,11 +382,11 @@ def tile_layer_simple_pa_t_kernel(
                 if j == 1:
                     sort_features(g + 1)
                 add_to_statistics(turn - STATISTICS_LAG)
+                transpose_operator(turn)
                 apply_operator(turn - STEP_1_LAG)
                 quantise_x1(turn - QUANTISE_X1_LAG)
                 if j == 2:
                     transpose_features(g + 1)
-                transpose_operator(turn)
                 convolve(turn - STEP_2_LAG)
                 if j == 0:
                     quantise_features(g)

@@ -26,7 +26,6 @@ EPS = 1e-5
 TILES = 4
 PAIRS = 2
 PAIR_COLS = 2 * P
-RUN = 16
 
 SORT_AHEAD = 1
 QUANTISE_W_LAG = 1
@@ -54,7 +53,7 @@ def tile_layer_simple_pa_t_kernel(
         bank_psum = pools.enter_context(tc.psum_pool(name="bank_psum", bufs=6))
         y_psum = pools.enter_context(tc.psum_pool(name="y_psum", bufs=CONVS))
 
-        w_raws, x_raws, x_sorteds, x_groupeds, x_operands, y_banks = {}, {}, {}, {}, {}, {}
+        w_raws, x_raws, x_groupeds, x_operands, y_banks = {}, {}, {}, {}, {}
         w_sorteds, w_groupeds, w_operands, x1_groupeds, x1_operands = {}, {}, {}, {}, {}
 
         def node_pieces(g):
@@ -80,7 +79,9 @@ def tile_layer_simple_pa_t_kernel(
             if g >= GRAPHS:
                 return
             x_raw = raw_pool.tile([P, TILES, NODES], BF16)
-            nc.sync.dma_start(out=x_raw[:], in_=X[g].rearrange("(m t) n -> m t n", t=TILES))
+            rows = X[g].rearrange("(m t) n -> m t n", t=TILES)
+            for tiles in pieces_of(g):
+                nc.sync.dma_start(out=x_raw[:, tiles, :], in_=rows[:, tiles, :])
             x_raws[g] = x_raw
 
         load_features(0)
@@ -90,8 +91,8 @@ def tile_layer_simple_pa_t_kernel(
             cv_raw = const.tile([P, CHANNELS], BF16, name="cv_raw%d" % len(cv_raws))
             nc.sync.dma_start(out=cv_raw[:], in_=cv_w)
             cv_raws.append(cv_raw)
-        load_operators(1)
         load_features(1)
+        load_operators(1)
 
         mask_all = const.tile([P, GRAPHS, NODES], BF16)
         nc.sync.dma_start(
@@ -139,6 +140,7 @@ def tile_layer_simple_pa_t_kernel(
         partial = const.tile([P, 2], F32)
         totals = const.tile([P, 2], F32)
         ratio_less_1 = const.tile([P, 1], F32)
+        beta_mask = const.tile([P, NODES], F32)
         preparation_banks = {}
 
         def prepare(step):
@@ -173,6 +175,14 @@ def tile_layer_simple_pa_t_kernel(
                 nc.vector.tensor_scalar_mul(out=offset_0[:], in0=bias, scalar1=ratio_less_1[:])
             elif step == 7:
                 nc.vector.tensor_scalar_mul(out=twice_offset_0[:], in0=offset_0[:], scalar1=2.0)
+                nc.gpsimd.tensor_scalar(
+                    out=beta_mask[:],
+                    in0=mask_all[:, 0, :],
+                    scalar1=beta[:, 0:1],
+                    scalar2=0.0,
+                    op0=ALU.mult,
+                    op1=ALU.add,
+                )
 
         zm = const.tile([P, CONVS, GRAPHS, NODES], F32)
         parts = const.tile([P, 2, CONVS, GRAPHS + 1], F32)
@@ -218,24 +228,13 @@ def tile_layer_simple_pa_t_kernel(
                 return
             g, j = divmod(unit, OPERATORS)
             w_sorted = unit_pool.tile([P, TILES, NODES], BF16)
-            by_operator = w_raws[g][:].rearrange("p i (q u c j) -> p i u q c j", u=2, c=RUN, j=OPERATORS)
-            by_half = w_sorted[:].rearrange("p i (u q c) -> p i u q c", u=2, c=RUN)
+            by_operator = w_raws[g][:].rearrange("p i (q u e j) -> p i q u e j", u=2, e=2, j=OPERATORS)
+            in_order = w_sorted[:].rearrange("p i (u q e) -> p i q u e", u=2, e=2)
             for tiles in pieces_of(g):
-                nc.vector.tensor_copy(out=by_half[:, tiles], in_=by_operator[:, tiles, :, :, :, j])
+                nc.vector.tensor_copy(out=in_order[:, tiles], in_=by_operator[:, tiles, :, :, :, j])
             w_sorteds[unit] = w_sorted
             if j == OPERATORS - 1:
                 load_operators(g + 2)
-
-        def sort_features(g):
-            if g >= GRAPHS:
-                return
-            x_sorted = graph_pool.tile([P, TILES, NODES], BF16)
-            nc.vector.tensor_copy(
-                out=x_sorted[:].rearrange("p i (u q c) -> p i u q c", u=2, c=RUN),
-                in_=x_raws[g][:].rearrange("p i (q u c) -> p i u q c", u=2, c=RUN),
-            )
-            x_sorteds[g] = x_sorted
-            load_features(g + 2)
 
         def transpose_features(g):
             if g >= GRAPHS:
@@ -244,12 +243,13 @@ def tile_layer_simple_pa_t_kernel(
             x_groupeds[g] = x_grouped
             for pair in range(PAIRS):
                 x_t = bank_psum.tile([P, 2, PAIR_COLS], F32, tag="bank")
-                transpose_words(x_t, lambda i: x_sorteds[g][:, 2 * pair + i, :], in_halves)
+                transpose_words(x_t, lambda i: x_raws[g][:, 2 * pair + i, :], stepped)
                 copy = nc.vector.tensor_copy if pair else nc.scalar.copy
                 copy(
                     out=x_grouped[:].bitcast(F32)[:, PAIR_COLS * pair : PAIR_COLS * (pair + 1), :],
                     in_=x_t[:].rearrange("p u c -> p c u"),
                 )
+            load_features(g + 2)
 
         def transpose_operator(unit):
             if not live(unit):
@@ -369,7 +369,6 @@ def tile_layer_simple_pa_t_kernel(
         with tc.manual_schedule(
             engines={mybir.EngineType.PE, mybir.EngineType.DVE, mybir.EngineType.Activation}
         ):
-            sort_features(0)
             sort_operator(0)
             transpose_features(0)
             transpose_operator(0)
@@ -379,8 +378,6 @@ def tile_layer_simple_pa_t_kernel(
                 g, j = divmod(turn, OPERATORS)
                 sort_operator(turn + SORT_AHEAD)
                 quantise_operator(turn - QUANTISE_W_LAG)
-                if j == 1:
-                    sort_features(g + 1)
                 add_to_statistics(turn - STATISTICS_LAG)
                 transpose_operator(turn)
                 apply_operator(turn - STEP_1_LAG)
@@ -422,6 +419,15 @@ def tile_layer_simple_pa_t_kernel(
                 op0=ALU.mult,
                 op1=ALU.add,
             )
+        first_piece = zm[:, 0, 0, :]
+        nc.vector.scalar_tensor_tensor(
+            out=first_piece,
+            in0=mask_all[:, 0, :],
+            scalar=neg_offset[:, 0:1],
+            in1=first_piece,
+            op0=ALU.mult,
+            op1=ALU.add,
+        )
         inv_std = const.tile([P, CONVS], F32)
         nc.scalar.activation(out=inv_std[:], in_=var[:], func=ACT.Abs_reciprocal_sqrt, bias=eps[:])
         gain = const.tile([P, CONVS], F32)
@@ -431,7 +437,7 @@ def tile_layer_simple_pa_t_kernel(
                 out=gain[:, column], in_=inv_std[:, column], func=ACT.Copy, scale=gamma[:, column]
             )
         shift = const.tile([P, CONVS], F32)
-        for conv in range(CONVS):
+        for conv in reversed(range(CONVS)):
             column = slice(conv, conv + 1)
             nc.scalar.activation(
                 out=shift[:, column],
@@ -441,22 +447,27 @@ def tile_layer_simple_pa_t_kernel(
                 bias=beta[:, column],
             )
 
+        def finish(conv, g, cols, term):
+            piece = zm[:, conv, g, cols]
+            nc.vector.scalar_tensor_tensor(
+                out=piece,
+                in0=piece,
+                scalar=gain[:, conv : conv + 1],
+                in1=term,
+                op0=ALU.mult,
+                op1=ALU.add,
+            )
+            nc.sync.dma_start(out=out[g, P * conv : P * (conv + 1), cols], in_=piece)
+
         for g in range(GRAPHS):
             for conv in range(CONVS):
-                half = NODES // 2
-                whole = [slice(0, NODES)]
-                for cols in [slice(0, half), slice(half, NODES)] if g == conv == 0 else whole:
-                    piece = zm[:, conv, g, cols]
+                if g == conv == 0:
+                    half = NODES // 2
+                    for cols in (slice(0, half), slice(half, NODES)):
+                        finish(conv, g, cols, beta_mask[:, cols])
+                else:
                     shifted = stat_pool.tile([P, NODES], F32)
                     nc.scalar.activation(
-                        out=shifted[:, cols], in_=mask_all[:, g, cols], func=ACT.Copy, scale=shift[:, conv : conv + 1]
+                        out=shifted[:], in_=mask_all[:, g, :], func=ACT.Copy, scale=shift[:, conv : conv + 1]
                     )
-                    nc.vector.scalar_tensor_tensor(
-                        out=piece,
-                        in0=piece,
-                        scalar=gain[:, conv : conv + 1],
-                        in1=shifted[:, cols],
-                        op0=ALU.mult,
-                        op1=ALU.add,
-                    )
-                    nc.sync.dma_start(out=out[g, P * conv : P * (conv + 1), cols], in_=piece)
+                    finish(conv, g, slice(0, NODES), shifted[:])

@@ -33,7 +33,7 @@ STEP_1_LAG = 2
 QUANTISE_X1_LAG = 3
 STEP_2_LAG = 4
 STATISTICS_LAG = 5
-CONV_WEIGHTS_TURN = 1
+CONV_WEIGHTS_TURN = 3
 PREPARATION_TURN = 2
 
 FLOPS = 2 * GRAPHS * (OPERATORS * NODES * NODES * FEATURES + CONVS * P * CHANNELS * NODES)
@@ -53,7 +53,7 @@ def tile_layer_simple_pa_t_kernel(
         bank_psum = pools.enter_context(tc.psum_pool(name="bank_psum", bufs=6))
         y_psum = pools.enter_context(tc.psum_pool(name="y_psum", bufs=CONVS))
 
-        w_raws, x_raws, x_groupeds, x_operands, y_banks = {}, {}, {}, {}, {}
+        w_raws, x_raws, x_banks, x_groupeds, x_operands, y_banks = {}, {}, {}, {}, {}, {}
         w_sorteds, w_groupeds, w_operands, x1_groupeds, x1_operands = {}, {}, {}, {}, {}
 
         def node_pieces(g):
@@ -64,7 +64,7 @@ def tile_layer_simple_pa_t_kernel(
             return 0 <= unit < UNITS
 
         def pieces_of(g):
-            return [slice(0, 2), slice(2, TILES)] if g == 0 else [slice(0, TILES)]
+            return [slice(i, i + 1) for i in range(TILES)] if g == 0 else [slice(0, TILES)]
 
         def load_operators(g):
             if g >= GRAPHS:
@@ -79,20 +79,18 @@ def tile_layer_simple_pa_t_kernel(
             if g >= GRAPHS:
                 return
             x_raw = raw_pool.tile([P, TILES, NODES], BF16)
-            rows = X[g].rearrange("(m t) n -> m t n", t=TILES)
-            for tiles in pieces_of(g):
-                nc.sync.dma_start(out=x_raw[:, tiles, :], in_=rows[:, tiles, :])
+            nc.sync.dma_start(out=x_raw[:], in_=X[g].rearrange("(m t) n -> m t n", t=TILES))
             x_raws[g] = x_raw
 
-        load_features(0)
         load_operators(0)
+        load_features(0)
+        load_operators(1)
+        load_features(1)
         cv_raws = []
         for cv_w in (cv2_w, cv1_w):
             cv_raw = const.tile([P, CHANNELS], BF16, name="cv_raw%d" % len(cv_raws))
             nc.sync.dma_start(out=cv_raw[:], in_=cv_w)
             cv_raws.append(cv_raw)
-        load_features(1)
-        load_operators(1)
 
         mask_all = const.tile([P, GRAPHS, NODES], BF16)
         nc.sync.dma_start(
@@ -133,9 +131,9 @@ def tile_layer_simple_pa_t_kernel(
 
         neg_bias = const.tile([P, CONVS], F32)
         inv_total = const.tile([P, 1], F32)
-        ratio_less_2 = const.tile([P, 1], F32)
+        inner_slope = const.tile([P, 1], F32)
         offset_0 = const.tile([P, CONVS], F32)
-        twice_offset_0 = const.tile([P, CONVS], F32)
+        inner_0 = const.tile([P, CONVS], F32)
 
         partial = const.tile([P, 2], F32)
         totals = const.tile([P, 2], F32)
@@ -171,10 +169,24 @@ def tile_layer_simple_pa_t_kernel(
                     op1=ALU.add,
                 )
             elif step == 6:
-                nc.vector.tensor_scalar_add(out=ratio_less_2[:], in0=ratio_less_1[:], scalar1=-1.0)
+                nc.vector.tensor_scalar(
+                    out=inner_slope[:],
+                    in0=ratio_less_1[:],
+                    scalar1=-1.0,
+                    scalar2=inv_total[:],
+                    op0=ALU.add,
+                    op1=ALU.mult,
+                )
                 nc.vector.tensor_scalar_mul(out=offset_0[:], in0=bias, scalar1=ratio_less_1[:])
             elif step == 7:
-                nc.vector.tensor_scalar_mul(out=twice_offset_0[:], in0=offset_0[:], scalar1=2.0)
+                nc.vector.scalar_tensor_tensor(
+                    out=inner_0[:],
+                    in0=offset_0[:],
+                    scalar=ratio_less_1[:],
+                    in1=offset_0[:],
+                    op0=ALU.mult,
+                    op1=ALU.add,
+                )
                 nc.gpsimd.tensor_scalar(
                     out=beta_mask[:],
                     in0=mask_all[:, 0, :],
@@ -223,17 +235,32 @@ def tile_layer_simple_pa_t_kernel(
                         ident_f32[:],
                     )
 
-        def sort_operator(unit):
-            if not live(unit):
+        def sort_operators(units, token=None):
+            g = units[0] // OPERATORS
+            if g >= GRAPHS:
                 return
-            g, j = divmod(unit, OPERATORS)
-            w_sorted = unit_pool.tile([P, TILES, NODES], BF16)
+            for unit in units:
+                w_sorted = unit_pool.tile([P, TILES, NODES], BF16)
+                w_sorteds[unit] = w_sorted
             by_operator = w_raws[g][:].rearrange("p i (q u e j) -> p i q u e j", u=2, e=2, j=OPERATORS)
-            in_order = w_sorted[:].rearrange("p i (u q e) -> p i q u e", u=2, e=2)
             for tiles in pieces_of(g):
-                nc.vector.tensor_copy(out=in_order[:, tiles], in_=by_operator[:, tiles, :, :, :, j])
-            w_sorteds[unit] = w_sorted
-            if j == OPERATORS - 1:
+                for unit in units:
+                    in_order = w_sorteds[unit][:].rearrange("p i (u q e) -> p i q u e", u=2, e=2)
+                    if token is None:
+                        nc.vector.tensor_copy(
+                            out=in_order[:, tiles], in_=by_operator[:, tiles, :, :, :, unit % OPERATORS]
+                        )
+                    else:
+                        for i in range(TILES):
+                            nc.gpsimd.tensor_scalar(
+                                out=in_order[:, i],
+                                in0=by_operator[:, i, :, :, :, unit % OPERATORS],
+                                scalar1=token[:],
+                                scalar2=0.0,
+                                op0=ALU.mult,
+                                op1=ALU.add,
+                            )
+            if units[-1] % OPERATORS == OPERATORS - 1:
                 load_operators(g + 2)
 
         def transpose_features(g):
@@ -241,15 +268,20 @@ def tile_layer_simple_pa_t_kernel(
                 return
             x_grouped = graph_pool.tile([P, FEATURES, PACK], BF16, align_bytes=64)
             x_groupeds[g] = x_grouped
+            x_banks[g] = []
             for pair in range(PAIRS):
                 x_t = bank_psum.tile([P, 2, PAIR_COLS], F32, tag="bank")
+                x_banks[g].append(x_t)
                 transpose_words(x_t, lambda i: x_raws[g][:, 2 * pair + i, :], stepped)
-                copy = nc.vector.tensor_copy if pair else nc.scalar.copy
-                copy(
-                    out=x_grouped[:].bitcast(F32)[:, PAIR_COLS * pair : PAIR_COLS * (pair + 1), :],
-                    in_=x_t[:].rearrange("p u c -> p c u"),
-                )
+            copy_features(g, 0, nc.scalar.copy)
             load_features(g + 2)
+
+        def copy_features(g, pair, copy):
+            if g < GRAPHS:
+                copy(
+                    out=x_groupeds[g][:].bitcast(F32)[:, PAIR_COLS * pair : PAIR_COLS * (pair + 1), :],
+                    in_=x_banks[g][pair][:].rearrange("p u c -> p c u"),
+                )
 
         def transpose_operator(unit):
             if not live(unit):
@@ -259,7 +291,8 @@ def tile_layer_simple_pa_t_kernel(
             for pair in range(PAIRS):
                 w_t = bank_psum.tile([P, 2, PAIR_COLS], F32, tag="bank")
                 transpose_words(w_t, lambda i: w_sorteds[unit][:, 2 * pair + i, :], in_halves)
-                nc.scalar.copy(
+                copy = nc.vector.tensor_copy if pair and unit + 1 in range(3 * OPERATORS, UNITS, OPERATORS) else nc.scalar.copy
+                copy(
                     out=w_grouped[:].bitcast(F32)[:, PAIR_COLS * pair : PAIR_COLS * (pair + 1), :],
                     in_=w_t[:].rearrange("p u c -> p c u"),
                 )
@@ -369,15 +402,25 @@ def tile_layer_simple_pa_t_kernel(
         with tc.manual_schedule(
             engines={mybir.EngineType.PE, mybir.EngineType.DVE, mybir.EngineType.Activation}
         ):
-            sort_operator(0)
-            transpose_features(0)
+            gpsimd_units = range(3 * OPERATORS, UNITS, OPERATORS)
+            sort_operators(range(OPERATORS))
             transpose_operator(0)
+            transpose_operator(1)
+            quantise_operator(0)
+            transpose_features(0)
+            copy_features(0, 1, nc.vector.tensor_copy)
             quantise_features(0)
-            sort_operator(1)
-            for turn in range(1, UNITS + STATISTICS_LAG):
+            for turn in range(2, UNITS + STATISTICS_LAG):
                 g, j = divmod(turn, OPERATORS)
-                sort_operator(turn + SORT_AHEAD)
+                if turn + SORT_AHEAD not in gpsimd_units:
+                    sort_operators([turn + SORT_AHEAD])
+                if j == 0:
+                    copy_features(g, 1, nc.vector.tensor_copy)
                 quantise_operator(turn - QUANTISE_W_LAG)
+                if turn + 2 in gpsimd_units:
+                    token = graph_pool.tile([P, 1], F32)
+                    nc.vector.memset(token[:], 1.0)
+                    sort_operators([turn + 2], token)
                 add_to_statistics(turn - STATISTICS_LAG)
                 transpose_operator(turn)
                 apply_operator(turn - STEP_1_LAG)
@@ -393,81 +436,84 @@ def tile_layer_simple_pa_t_kernel(
                     quantise_conv_weights()
                 prepare(turn - PREPARATION_TURN)
 
-        sums = const.tile([P, 2 * CONVS], F32)
-        nc.vector.reduce_sum(out=sums[:], in_=parts[:].rearrange("p s c k -> p (s c) k"), axis=AXIS_X)
-        first, second = sums[:, 0:CONVS], sums[:, CONVS : 2 * CONVS]
-        offset = const.tile([P, CONVS], F32)
-        nc.vector.scalar_tensor_tensor(
-            out=offset[:], in0=first, scalar=inv_total[:], in1=offset_0[:], op0=ALU.mult, op1=ALU.add
-        )
-        mean_square = const.tile([P, CONVS], F32)
-        nc.vector.tensor_scalar_mul(out=mean_square[:], in0=second, scalar1=inv_total[:])
-        inner = const.tile([P, CONVS], F32)
-        nc.vector.scalar_tensor_tensor(
-            out=inner[:], in0=offset[:], scalar=ratio_less_2[:], in1=twice_offset_0[:], op0=ALU.mult, op1=ALU.add
-        )
-        neg_offset = const.tile([P, CONVS], F32)
-        nc.vector.tensor_scalar_mul(out=neg_offset[:], in0=offset[:], scalar1=-1.0)
-        var = const.tile([P, CONVS], F32)
-        for conv in range(CONVS):
-            column = slice(conv, conv + 1)
+        with tc.manual_schedule(
+            engines={mybir.EngineType.PE, mybir.EngineType.DVE, mybir.EngineType.Activation}
+        ):
+            sums = const.tile([P, 2 * CONVS], F32)
+            nc.vector.reduce_sum(out=sums[:], in_=parts[:].rearrange("p s c k -> p (s c) k"), axis=AXIS_X)
+            first, second = sums[:, 0:CONVS], sums[:, CONVS : 2 * CONVS]
+            offset = const.tile([P, CONVS], F32)
             nc.vector.scalar_tensor_tensor(
-                out=var[:, column],
-                in0=inner[:, column],
-                scalar=offset[:, column],
-                in1=mean_square[:, column],
-                op0=ALU.mult,
-                op1=ALU.add,
+                out=offset[:], in0=first, scalar=inv_total[:], in1=offset_0[:], op0=ALU.mult, op1=ALU.add
             )
-        first_piece = zm[:, 0, 0, :]
-        nc.vector.scalar_tensor_tensor(
-            out=first_piece,
-            in0=mask_all[:, 0, :],
-            scalar=neg_offset[:, 0:1],
-            in1=first_piece,
-            op0=ALU.mult,
-            op1=ALU.add,
-        )
-        inv_std = const.tile([P, CONVS], F32)
-        nc.scalar.activation(out=inv_std[:], in_=var[:], func=ACT.Abs_reciprocal_sqrt, bias=eps[:])
-        gain = const.tile([P, CONVS], F32)
-        for conv in range(CONVS):
-            column = slice(conv, conv + 1)
-            nc.scalar.activation(
-                out=gain[:, column], in_=inv_std[:, column], func=ACT.Copy, scale=gamma[:, column]
-            )
-        shift = const.tile([P, CONVS], F32)
-        for conv in reversed(range(CONVS)):
-            column = slice(conv, conv + 1)
-            nc.scalar.activation(
-                out=shift[:, column],
-                in_=gain[:, column],
-                func=ACT.Identity,
-                scale=neg_offset[:, column],
-                bias=beta[:, column],
-            )
-
-        def finish(conv, g, cols, term):
-            piece = zm[:, conv, g, cols]
+            mean_square = const.tile([P, CONVS], F32)
+            nc.vector.tensor_scalar_mul(out=mean_square[:], in0=second, scalar1=inv_total[:])
+            inner = const.tile([P, CONVS], F32)
             nc.vector.scalar_tensor_tensor(
-                out=piece,
-                in0=piece,
-                scalar=gain[:, conv : conv + 1],
-                in1=term,
-                op0=ALU.mult,
-                op1=ALU.add,
+                out=inner[:], in0=first, scalar=inner_slope[:], in1=inner_0[:], op0=ALU.mult, op1=ALU.add
             )
-            nc.sync.dma_start(out=out[g, P * conv : P * (conv + 1), cols], in_=piece)
-
-        for g in range(GRAPHS):
+            neg_offset = const.tile([P, CONVS], F32)
+            nc.vector.tensor_scalar_mul(out=neg_offset[:], in0=offset[:], scalar1=-1.0)
+            var = const.tile([P, CONVS], F32)
             for conv in range(CONVS):
-                if g == conv == 0:
-                    half = NODES // 2
-                    for cols in (slice(0, half), slice(half, NODES)):
-                        finish(conv, g, cols, beta_mask[:, cols])
-                else:
-                    shifted = stat_pool.tile([P, NODES], F32)
-                    nc.scalar.activation(
-                        out=shifted[:], in_=mask_all[:, g, :], func=ACT.Copy, scale=shift[:, conv : conv + 1]
-                    )
-                    finish(conv, g, slice(0, NODES), shifted[:])
+                column = slice(conv, conv + 1)
+                nc.vector.scalar_tensor_tensor(
+                    out=var[:, column],
+                    in0=inner[:, column],
+                    scalar=offset[:, column],
+                    in1=mean_square[:, column],
+                    op0=ALU.mult,
+                    op1=ALU.add,
+                )
+            first_piece = zm[:, 0, 0, :]
+            nc.vector.scalar_tensor_tensor(
+                out=first_piece,
+                in0=mask_all[:, 0, :],
+                scalar=neg_offset[:, 0:1],
+                in1=first_piece,
+                op0=ALU.mult,
+                op1=ALU.add,
+            )
+            inv_std = const.tile([P, CONVS], F32)
+            nc.scalar.activation(out=inv_std[:], in_=var[:], func=ACT.Abs_reciprocal_sqrt, bias=eps[:])
+            gain = const.tile([P, CONVS], F32)
+            for conv in range(CONVS):
+                column = slice(conv, conv + 1)
+                nc.scalar.activation(
+                    out=gain[:, column], in_=inv_std[:, column], func=ACT.Copy, scale=gamma[:, column]
+                )
+            shift = const.tile([P, CONVS], F32)
+            for conv in reversed(range(CONVS)):
+                column = slice(conv, conv + 1)
+                nc.scalar.activation(
+                    out=shift[:, column],
+                    in_=gain[:, column],
+                    func=ACT.Identity,
+                    scale=neg_offset[:, column],
+                    bias=beta[:, column],
+                )
+
+            def finish(conv, g, cols, term):
+                piece = zm[:, conv, g, cols]
+                nc.vector.scalar_tensor_tensor(
+                    out=piece,
+                    in0=piece,
+                    scalar=gain[:, conv : conv + 1],
+                    in1=term,
+                    op0=ALU.mult,
+                    op1=ALU.add,
+                )
+                nc.sync.dma_start(out=out[g, P * conv : P * (conv + 1), cols], in_=piece)
+
+            for g in range(GRAPHS):
+                for conv in range(CONVS):
+                    if g == conv == 0:
+                        half = NODES // 2
+                        for cols in (slice(0, half), slice(half, NODES)):
+                            finish(conv, g, cols, beta_mask[:, cols])
+                    else:
+                        shifted = stat_pool.tile([P, NODES], F32)
+                        nc.scalar.activation(
+                            out=shifted[:], in_=mask_all[:, g, :], func=ACT.Copy, scale=shift[:, conv : conv + 1]
+                        )
+                        finish(conv, g, slice(0, NODES), shifted[:])

from contextlib import ExitStack

import concourse.mybir as mybir
from concourse.masks import make_identity

F32 = mybir.dt.float32
BF16 = mybir.dt.bfloat16
U32 = mybir.dt.uint32
U8 = mybir.dt.uint8
FP8X4 = mybir.dt.float8_e4m3fn_x4
ALU = mybir.AluOpType
ACT = mybir.ActivationFunctionType
AXIS_X = mybir.AxisListType.X

P = 128
PACK = 4
GRAPHS = 8
FEATURES = 512
NODES = 512
OPERATORS = 3
UNITS = GRAPHS * OPERATORS
CONVS = 2
CHANNELS = OPERATORS * FEATURES
EPS = 1e-5

TILES = 4
PAIRS = 2
PAIR_COLS = 2 * P

SORT_AHEAD = 1
QUANTISE_W_LAG = 1
STEP_1_LAG = 2
QUANTISE_X1_LAG = 3
STEP_2_LAG = 4
STATISTICS_LAG = 5
CONV_WEIGHTS_TURN = 3
PREPARATION_TURN = 2

FLOPS = 2 * GRAPHS * (OPERATORS * NODES * NODES * FEATURES + CONVS * P * CHANNELS * NODES)


def tile_layer_simple_pa_t_kernel(
    tc, X, W, N_batch, mask, cv1_w, cv1_b, cv2_w, cv2_b, bn_gamma, bn_beta, out
):
    nc = tc.nc
    with ExitStack() as pools:
        const = pools.enter_context(tc.tile_pool(name="const", bufs=1))
        raw_pool = pools.enter_context(tc.tile_pool(name="raw", bufs=2))
        unit_pool = pools.enter_context(tc.tile_pool(name="unit", bufs=3))
        x1_pool = pools.enter_context(tc.tile_pool(name="x1", bufs=2 * OPERATORS))
        graph_pool = pools.enter_context(tc.tile_pool(name="graph", bufs=2))
        stat_pool = pools.enter_context(tc.tile_pool(name="stat", bufs=4))
        bank_psum = pools.enter_context(tc.psum_pool(name="bank_psum", bufs=6))
        y_psum = pools.enter_context(tc.psum_pool(name="y_psum", bufs=CONVS))

        w_raws, x_raws, x_banks, x_groupeds, x_operands, y_banks = {}, {}, {}, {}, {}, {}
        w_sorteds, w_groupeds, w_operands, x1_groupeds, x1_operands = {}, {}, {}, {}, {}

        def node_pieces(g):
            half = NODES // 2
            return [slice(0, half), slice(half, NODES)] if g == GRAPHS - 1 else [slice(0, NODES)]

        def live(unit):
            return 0 <= unit < UNITS

        def pieces_of(g):
            return [slice(i, i + 1) for i in range(TILES)] if g == 0 else [slice(0, TILES)]

        def load_operators(g):
            if g >= GRAPHS:
                return
            w_raw = raw_pool.tile([P, TILES, NODES * OPERATORS], BF16)
            rows = W[g].rearrange("(i p) n j -> p i (n j)", p=P)
            for tiles in pieces_of(g):
                nc.sync.dma_start(out=w_raw[:, tiles, :], in_=rows[:, tiles, :])
            w_raws[g] = w_raw

        def load_features(g):
            if g >= GRAPHS:
                return
            x_raw = raw_pool.tile([P, TILES, NODES], BF16)
            nc.sync.dma_start(out=x_raw[:], in_=X[g].rearrange("(m t) n -> m t n", t=TILES))
            x_raws[g] = x_raw

        load_operators(0)
        load_features(0)
        load_operators(1)
        load_features(1)
        cv_raws = []
        for cv_w in (cv2_w, cv1_w):
            cv_raw = const.tile([P, CHANNELS], BF16, name="cv_raw%d" % len(cv_raws))
            nc.sync.dma_start(out=cv_raw[:], in_=cv_w)
            cv_raws.append(cv_raw)

        mask_all = const.tile([P, GRAPHS, NODES], BF16)
        nc.sync.dma_start(
            out=mask_all[:].rearrange("p g m -> p (g m)"),
            in_=mask.rearrange("g o m -> (g o m)").partition_broadcast(P),
        )

        ident_f32 = const.tile([P, P], F32)
        make_identity(nc, ident_f32[:])
        ident_bf16 = const.tile([P, P], BF16)
        make_identity(nc, ident_bf16[:])
        ones_f32 = const.tile([P, P], F32)
        nc.vector.memset(ones_f32[:], 1.0)
        eps = const.tile([P, 1], F32)
        nc.vector.memset(eps[:], EPS)

        warm = const.tile([P, 1], F32)
        nc.scalar.activation(out=warm[:], in_=eps[:], func=ACT.Abs_reciprocal_sqrt)

        vector_rows = const.tile([P, P], BF16)
        nc.vector.memset(vector_rows[:], 0.0)
        nc.scalar.dma_start(out=vector_rows[0:1, :], in_=cv2_b.unsqueeze(0))
        nc.scalar.dma_start(out=vector_rows[1:2, :], in_=cv1_b.unsqueeze(0))
        nc.scalar.dma_start(out=vector_rows[2:4, :], in_=bn_gamma.rearrange("(h c) -> h c", h=CONVS))
        nc.scalar.dma_start(out=vector_rows[4:6, :], in_=bn_beta.rearrange("(h c) -> h c", h=CONVS))
        per_channel = const.tile([P, 3 * CONVS], F32)
        bias = per_channel[:, 0:CONVS]
        gamma = per_channel[:, CONVS : 2 * CONVS]
        beta = per_channel[:, 2 * CONVS : 3 * CONVS]

        mask_part = const.tile([P, GRAPHS * NODES // P], BF16)
        nc.scalar.dma_start(
            out=mask_part[:], in_=mask.rearrange("g o (q r) -> (g o q) r", r=GRAPHS * NODES // P)
        )
        counts_row = const.tile([P, GRAPHS], BF16)
        nc.vector.memset(counts_row[:], 0.0)
        nc.scalar.dma_start(out=counts_row[0:1, :], in_=N_batch.unsqueeze(0))

        neg_bias = const.tile([P, CONVS], F32)
        inv_total = const.tile([P, 1], F32)
        inner_slope = const.tile([P, 1], F32)
        offset_0 = const.tile([P, CONVS], F32)
        inner_0 = const.tile([P, CONVS], F32)

        partial = const.tile([P, 2], F32)
        totals = const.tile([P, 2], F32)
        ratio_less_1 = const.tile([P, 1], F32)
        beta_mask = const.tile([P, NODES], F32)
        preparation_banks = {}

        def prepare(step):
            if step == 0:
                vector_cols = bank_psum.tile([P, P], BF16, tag="bank")
                nc.tensor.transpose(vector_cols[:], vector_rows[:], ident_bf16[:])
                preparation_banks["vectors"] = vector_cols
                nc.vector.reduce_sum(out=partial[:, 0:1], in_=mask_part[:], axis=AXIS_X)
            elif step == 1:
                nc.vector.tensor_copy(out=per_channel[:], in_=preparation_banks["vectors"][:, 0 : 3 * CONVS])
                nc.vector.reduce_sum(out=partial[:, 1:2], in_=counts_row[:], axis=AXIS_X)
            elif step == 2:
                totals_psum = bank_psum.tile([P, 2], F32, tag="bank")
                nc.tensor.matmul(out=totals_psum[:], lhsT=ones_f32[:], rhs=partial[:], start=True, stop=True)
                preparation_banks["totals"] = totals_psum
                nc.vector.tensor_scalar_mul(out=neg_bias[:], in0=bias, scalar1=-1.0)
            elif step == 3:
                nc.vector.tensor_copy(out=totals[:], in_=preparation_banks["totals"][:])
            elif step == 4:
                nc.vector.reciprocal(out=inv_total[:], in_=totals[:, 1:2])
            elif step == 5:
                nc.vector.tensor_scalar(
                    out=ratio_less_1[:],
                    in0=totals[:, 0:1],
                    scalar1=inv_total[:],
                    scalar2=-1.0,
                    op0=ALU.mult,
                    op1=ALU.add,
                )
            elif step == 6:
                nc.vector.tensor_scalar(
                    out=inner_slope[:],
                    in0=ratio_less_1[:],
                    scalar1=-1.0,
                    scalar2=inv_total[:],
                    op0=ALU.add,
                    op1=ALU.mult,
                )
                nc.vector.tensor_scalar_mul(out=offset_0[:], in0=bias, scalar1=ratio_less_1[:])
            elif step == 7:
                nc.vector.scalar_tensor_tensor(
                    out=inner_0[:],
                    in0=offset_0[:],
                    scalar=ratio_less_1[:],
                    in1=offset_0[:],
                    op0=ALU.mult,
                    op1=ALU.add,
                )
                nc.gpsimd.tensor_scalar(
                    out=beta_mask[:],
                    in0=mask_all[:, 0, :],
                    scalar1=beta[:, 0:1],
                    scalar2=0.0,
                    op0=ALU.mult,
                    op1=ALU.add,
                )

        zm = const.tile([P, CONVS, GRAPHS, NODES], F32)
        parts = const.tile([P, 2, CONVS, GRAPHS + 1], F32)

        cv_grouped = const.tile([P, OPERATORS, PAIR_COLS, PACK], BF16, align_bytes=64)
        cv_codes = const.tile([P, OPERATORS, PAIR_COLS], U32, align_bytes=64)
        cv_scales = const.tile([P, OPERATORS, PAIR_COLS], U8, align_bytes=64)

        def transpose_conv_weights():
            for j in range(OPERATORS):
                cv_t = bank_psum.tile([P, 2, PAIR_COLS], F32, tag="bank")
                transpose_words(cv_t, lambda i: cv_raws[i][:, FEATURES * j : FEATURES * (j + 1)], stepped)
                nc.scalar.copy(
                    out=cv_grouped[:, j].rearrange("p o t -> p (o t)").bitcast(F32).rearrange("p (o u) -> p o u", u=2),
                    in_=cv_t[:].rearrange("p u c -> p c u"),
                )

        def quantise_conv_weights():
            for j in range(OPERATORS):
                nc.vector.quantize_mx(
                    out=cv_codes[:, j, :].bitcast(FP8X4),
                    scales=cv_scales[:, j, :],
                    in_=cv_grouped[:, j].rearrange("p o t -> p (o t)"),
                )

        def stepped(u):
            return slice(u, 2 * P, 2)

        def in_halves(u):
            return slice(P * u, P * (u + 1))

        def transpose_words(bank, rows_of, words_of):
            for u in range(2):
                for i in range(2):
                    nc.tensor.transpose(
                        bank[:, u, P * i : P * (i + 1)],
                        rows_of(i).bitcast(F32)[:, words_of(u)],
                        ident_f32[:],
                    )

        def sort_operators(units, token=None):
            g = units[0] // OPERATORS
            if g >= GRAPHS:
                return
            for unit in units:
                w_sorted = unit_pool.tile([P, TILES, NODES], BF16)
                w_sorteds[unit] = w_sorted
            by_operator = w_raws[g][:].rearrange("p i (q u e j) -> p i q u e j", u=2, e=2, j=OPERATORS)
            for tiles in pieces_of(g):
                for unit in units:
                    in_order = w_sorteds[unit][:].rearrange("p i (u q e) -> p i q u e", u=2, e=2)
                    if token is None:
                        nc.vector.tensor_copy(
                            out=in_order[:, tiles], in_=by_operator[:, tiles, :, :, :, unit % OPERATORS]
                        )
                    else:
                        for i in range(TILES):
                            nc.gpsimd.tensor_scalar(
                                out=in_order[:, i],
                                in0=by_operator[:, i, :, :, :, unit % OPERATORS],
                                scalar1=token[:],
                                scalar2=0.0,
                                op0=ALU.mult,
                                op1=ALU.add,
                            )
            if units[-1] % OPERATORS == OPERATORS - 1:
                load_operators(g + 2)

        def transpose_features(g):
            if g >= GRAPHS:
                return
            x_grouped = graph_pool.tile([P, FEATURES, PACK], BF16, align_bytes=64)
            x_groupeds[g] = x_grouped
            x_banks[g] = []
            for pair in range(PAIRS):
                x_t = bank_psum.tile([P, 2, PAIR_COLS], F32, tag="bank")
                x_banks[g].append(x_t)
                transpose_words(x_t, lambda i: x_raws[g][:, 2 * pair + i, :], stepped)
            copy_features(g, 0, nc.scalar.copy)
            load_features(g + 2)

        def copy_features(g, pair, copy):
            if g < GRAPHS:
                copy(
                    out=x_groupeds[g][:].bitcast(F32)[:, PAIR_COLS * pair : PAIR_COLS * (pair + 1), :],
                    in_=x_banks[g][pair][:].rearrange("p u c -> p c u"),
                )

        def transpose_operator(unit):
            if not live(unit):
                return
            w_grouped = unit_pool.tile([P, NODES, PACK], BF16, align_bytes=64)
            w_groupeds[unit] = w_grouped
            for pair in range(PAIRS):
                w_t = bank_psum.tile([P, 2, PAIR_COLS], F32, tag="bank")
                transpose_words(w_t, lambda i: w_sorteds[unit][:, 2 * pair + i, :], in_halves)
                copy = nc.vector.tensor_copy if pair and unit + 1 in range(3 * OPERATORS, UNITS, OPERATORS) else nc.scalar.copy
                copy(
                    out=w_grouped[:].bitcast(F32)[:, PAIR_COLS * pair : PAIR_COLS * (pair + 1), :],
                    in_=w_t[:].rearrange("p u c -> p c u"),
                )

        def quantise(grouped, pool, kind, pieces=(slice(0, NODES),)):
            codes = pool.tile([P, NODES], U32, align_bytes=64, name=kind + "_codes")
            scales = pool.tile([P, NODES], U8, align_bytes=64, name=kind + "_scales")
            for cols in pieces:
                nc.vector.quantize_mx(
                    out=codes[:, cols].bitcast(FP8X4),
                    scales=scales[:, cols],
                    in_=grouped[:, cols, :].rearrange("p c t -> p (c t)"),
                )
            return codes, scales

        def quantise_features(g):
            if g < GRAPHS:
                x_operands[g] = quantise(x_groupeds[g], graph_pool, "x")

        def quantise_operator(unit):
            if live(unit):
                w_operands[unit] = quantise(w_groupeds[unit], unit_pool, "w")

        def apply_operator(unit):
            if not live(unit):
                return
            x_codes, x_scales = x_operands[unit // OPERATORS]
            w_codes, w_scales = w_operands[unit]
            x1_grouped = unit_pool.tile([P, NODES, PACK], BF16, align_bytes=64)
            x1_groupeds[unit] = x1_grouped
            for i in range(TILES):
                m_cols = slice(P * i, P * (i + 1))
                x1_bank = bank_psum.tile([P, PACK, P], F32, tag="bank")
                for t in range(PACK):
                    f_cols = slice(P * t, P * (t + 1))
                    nc.tensor.matmul_mx(
                        out=x1_bank[:, t, :],
                        lhsT=x_codes[:, f_cols].bitcast(FP8X4),
                        lhsT_scale=x_scales[:, f_cols],
                        rhs=w_codes[:, m_cols].bitcast(FP8X4),
                        rhs_scale=w_scales[:, m_cols],
                        start=True,
                        stop=True,
                    )
                nc.scalar.copy(out=x1_grouped[:, m_cols, :], in_=x1_bank[:].rearrange("p t m -> p m t"))

        def quantise_x1(unit):
            if live(unit):
                pieces = node_pieces(unit // OPERATORS) if unit == UNITS - 1 else [slice(0, NODES)]
                x1_operands[unit] = quantise(x1_groupeds[unit], x1_pool, "x1", pieces)

        def convolve(unit):
            if not live(unit):
                return
            g, j = divmod(unit, OPERATORS)
            last = g == GRAPHS - 1
            if j < OPERATORS - 1 and not last:
                return
            for piece, cols in enumerate(node_pieces(g)):
                for conv in range(CONVS):
                    if (g, conv, piece) not in y_banks:
                        if piece == 0:
                            y = y_psum.tile([P, NODES], F32, tag="y")
                        else:
                            y = bank_psum.tile([P, NODES], F32, tag="bank")
                        y_banks[g, conv, piece] = y[:, 0 : cols.stop - cols.start]
                    for operator in [j] if last else range(OPERATORS):
                        x1_codes, x1_scales = x1_operands[OPERATORS * g + operator]
                        nc.tensor.matmul_mx(
                            out=y_banks[g, conv, piece],
                            lhsT=cv_codes[:, operator, P * conv : P * (conv + 1)].bitcast(FP8X4),
                            lhsT_scale=cv_scales[:, operator, P * conv : P * (conv + 1)],
                            rhs=x1_codes[:, cols].bitcast(FP8X4),
                            rhs_scale=x1_scales[:, cols],
                            start=(operator == 0),
                            stop=(operator == OPERATORS - 1),
                        )

        def add_to_statistics(unit):
            g, j = divmod(unit, OPERATORS)
            if not live(unit) or j != OPERATORS - 1:
                return
            for piece, cols in enumerate(node_pieces(g)):
                part = g + piece
                for conv in range(CONVS):
                    nc.vector.scalar_tensor_tensor(
                        out=zm[:, conv, g, cols],
                        in0=y_banks[g, conv, piece],
                        scalar=neg_bias[:, conv : conv + 1],
                        in1=mask_all[:, g, cols],
                        op0=ALU.max,
                        op1=ALU.mult,
                        accum_out=parts[:, 0, conv, part : part + 1],
                    )
                for conv in range(CONVS):
                    squares = stat_pool.tile([P, NODES], F32)
                    nc.vector.scalar_tensor_tensor(
                        out=squares[:, cols],
                        in0=y_banks[g, conv, piece],
                        scalar=neg_bias[:, conv : conv + 1],
                        in1=zm[:, conv, g, cols],
                        op0=ALU.max,
                        op1=ALU.mult,
                        accum_out=parts[:, 1, conv, part : part + 1],
                    )

        with tc.manual_schedule(
            engines={mybir.EngineType.PE, mybir.EngineType.DVE, mybir.EngineType.Activation}
        ):
            gpsimd_units = range(3 * OPERATORS, UNITS, OPERATORS)
            sort_operators(range(OPERATORS))
            transpose_operator(0)
            transpose_operator(1)
            quantise_operator(0)
            transpose_features(0)
            copy_features(0, 1, nc.vector.tensor_copy)
            quantise_features(0)
            for turn in range(2, UNITS + STATISTICS_LAG):
                g, j = divmod(turn, OPERATORS)
                if turn + SORT_AHEAD not in gpsimd_units:
                    sort_operators([turn + SORT_AHEAD])
                if j == 0:
                    copy_features(g, 1, nc.vector.tensor_copy)
                quantise_operator(turn - QUANTISE_W_LAG)
                if turn + 2 in gpsimd_units:
                    token = graph_pool.tile([P, 1], F32)
                    nc.vector.memset(token[:], 1.0)
                    sort_operators([turn + 2], token)
                add_to_statistics(turn - STATISTICS_LAG)
                transpose_operator(turn)
                apply_operator(turn - STEP_1_LAG)
                quantise_x1(turn - QUANTISE_X1_LAG)
                if j == 2:
                    transpose_features(g + 1)
                convolve(turn - STEP_2_LAG)
                if j == 0:
                    quantise_features(g)
                if turn == CONV_WEIGHTS_TURN:
                    transpose_conv_weights()
                if turn == CONV_WEIGHTS_TURN + 2:
                    quantise_conv_weights()
                prepare(turn - PREPARATION_TURN)

        with tc.manual_schedule(
            engines={mybir.EngineType.PE, mybir.EngineType.DVE, mybir.EngineType.Activation}
        ):
            sums = const.tile([P, 2 * CONVS], F32)
            nc.vector.reduce_sum(out=sums[:], in_=parts[:].rearrange("p s c k -> p (s c) k"), axis=AXIS_X)
            first, second = sums[:, 0:CONVS], sums[:, CONVS : 2 * CONVS]
            offset = const.tile([P, CONVS], F32)
            nc.vector.scalar_tensor_tensor(
                out=offset[:], in0=first, scalar=inv_total[:], in1=offset_0[:], op0=ALU.mult, op1=ALU.add
            )
            mean_square = const.tile([P, CONVS], F32)
            nc.vector.tensor_scalar_mul(out=mean_square[:], in0=second, scalar1=inv_total[:])
            inner = const.tile([P, CONVS], F32)
            nc.vector.scalar_tensor_tensor(
                out=inner[:], in0=first, scalar=inner_slope[:], in1=inner_0[:], op0=ALU.mult, op1=ALU.add
            )
            neg_offset = const.tile([P, CONVS], F32)
            nc.vector.tensor_scalar_mul(out=neg_offset[:], in0=offset[:], scalar1=-1.0)
            var = const.tile([P, CONVS], F32)
            for conv in range(CONVS):
                column = slice(conv, conv + 1)
                nc.vector.scalar_tensor_tensor(
                    out=var[:, column],
                    in0=inner[:, column],
                    scalar=offset[:, column],
                    in1=mean_square[:, column],
                    op0=ALU.mult,
                    op1=ALU.add,
                )
            first_piece = zm[:, 0, 0, :]
            nc.vector.scalar_tensor_tensor(
                out=first_piece,
                in0=mask_all[:, 0, :],
                scalar=neg_offset[:, 0:1],
                in1=first_piece,
                op0=ALU.mult,
                op1=ALU.add,
            )
            inv_std = const.tile([P, CONVS], F32)
            nc.scalar.activation(out=inv_std[:], in_=var[:], func=ACT.Abs_reciprocal_sqrt, bias=eps[:])
            gain = const.tile([P, CONVS], F32)
            for conv in range(CONVS):
                column = slice(conv, conv + 1)
                nc.scalar.activation(
                    out=gain[:, column], in_=inv_std[:, column], func=ACT.Copy, scale=gamma[:, column]
                )
            shift = const.tile([P, CONVS], F32)
            for conv in reversed(range(CONVS)):
                column = slice(conv, conv + 1)
                nc.scalar.activation(
                    out=shift[:, column],
                    in_=gain[:, column],
                    func=ACT.Identity,
                    scale=neg_offset[:, column],
                    bias=beta[:, column],
                )

            def finish(conv, g, cols, term):
                piece = zm[:, conv, g, cols]
                nc.vector.scalar_tensor_tensor(
                    out=piece,
                    in0=piece,
                    scalar=gain[:, conv : conv + 1],
                    in1=term,
                    op0=ALU.mult,
                    op1=ALU.add,
                )
                nc.sync.dma_start(out=out[g, P * conv : P * (conv + 1), cols], in_=piece)

            for g in range(GRAPHS):
                for conv in range(CONVS):
                    if g == conv == 0:
                        half = NODES // 2
                        for cols in (slice(0, half), slice(half, NODES)):
                            finish(conv, g, cols, beta_mask[:, cols])
                    else:
                        shifted = stat_pool.tile([P, NODES], F32)
                        nc.scalar.activation(
                            out=shifted[:], in_=mask_all[:, g, :], func=ACT.Copy, scale=shift[:, conv : conv + 1]
                        )
                        finish(conv, g, slice(0, NODES), shifted[:])
